import numpy as np
import ml_dtypes


def mxq(x, axis, fmt="e4m3"):
    dtype, down = {"e4m3": (ml_dtypes.float8_e4m3fn, 7), "e5m2": (ml_dtypes.float8_e5m2, 14)}[fmt]
    v = np.moveaxis(np.asarray(x, np.float32).astype(ml_dtypes.bfloat16).astype(np.float64), axis, -1)
    blocks = v.reshape(v.shape[:-1] + (-1, 32))
    amax = np.abs(blocks).max(-1, keepdims=True)
    byte = np.maximum(np.where(amax > 0, np.frexp(amax)[1] - 1 + 127, 0) - down, 1)
    scale = np.exp2(byte - 127.0)
    codes = (blocks / scale).astype(np.float32).astype(dtype).astype(np.float64)
    return np.moveaxis((codes * scale).reshape(v.shape), -1, axis)


WIDE = False


def mx_kscale(k):
    if not WIDE:
        return np.ones(k)
    levels = np.array([30, -30])
    if k % 512:
        return np.exp2(np.random.permutation(np.resize(levels, k // 32))).repeat(32)
    a = np.empty((k // 512, 16))
    for p in range(k // 512):
        a[p, :8] = np.random.permutation(np.resize(levels, 8))
        for g in range(8):
            far = levels[np.abs(levels - a[p, g]) >= 10]
            a[p, g + 8] = far[np.random.randint(len(far))]
    return np.exp2(a.ravel()).repeat(32)


BF16 = ml_dtypes.bfloat16


def bf(x):
    return np.asarray(x, np.float32).astype(BF16)


def f64(x):
    return np.asarray(x).astype(np.float64)


E2M1 = np.array([0.0, 0.5, 1.0, 1.5, 2.0, 3.0, 4.0, 6.0, -0.0, -0.5, -1.0, -1.5, -2.0, -3.0, -4.0, -6.0])


def pack_weight(w, fmt):
    k, n = w.shape
    w = f64(bf(w)).reshape(k // 32, 32, n)
    amax = np.abs(w).max(1)
    if fmt == "e4m3":
        byte = np.frexp(amax)[1] - 1 + 127 - 7
    else:
        mant, ex = np.frexp(amax / 6.0)
        byte = np.where(mant > 0.5, ex, ex - 1) + 127
    byte = np.clip(np.where(amax > 0, byte, 1), 1, 254)
    scaled = (w * np.exp2(127.0 - byte)[:, None, :]).reshape(k, n).astype(np.float32)
    by_word = np.ascontiguousarray(scaled.reshape(k // 512, 128, 4, n).transpose(0, 1, 3, 2))
    if fmt == "e4m3":
        words = by_word.astype(ml_dtypes.float8_e4m3fn).view(np.uint8)
    else:
        c = by_word.astype(ml_dtypes.float4_e2m1fn).view(np.uint8) & 0xF
        words = c[..., 0::2] | (c[..., 1::2] << 4)
    return np.ascontiguousarray(words), np.ascontiguousarray(byte.astype(np.uint8).reshape(k // 512, 16, n))


def unpack_weight(words, scales, fmt):
    g, p, n, _ = words.shape
    if fmt == "e4m3":
        vals = np.ascontiguousarray(words).view(ml_dtypes.float8_e4m3fn).astype(np.float64)
    else:
        nib = np.empty((g, p, n, 4), np.uint8)
        nib[..., 0::2] = words & 0xF
        nib[..., 1::2] = words >> 4
        vals = E2M1[nib]
    vals = vals * np.repeat(np.exp2(scales.astype(np.float64) - 127.0), 8, axis=1)[..., None]
    return vals.transpose(0, 1, 3, 2).reshape(g * 512, n)

def pack4(w):
    words, scales = pack_weight(w, "e2m1")
    return words.reshape(words.shape[0], 128, -1), scales


def unpack4(words, scales):
    return unpack_weight(words.reshape(words.shape[0], 128, -1, 2), scales, "e2m1")


N, C, H = 512, 2048, 16
D = C // H
SIN_TIME = 10000.0


def create_sinusoidal_positions(n_pos, dim, time):
    denom = np.power(time, 2 * (np.arange(dim) // 2) / dim)
    position_enc = np.arange(n_pos)[:, None] / denom[None, :]
    return np.concatenate([np.sin(position_enc[:, 0::2]), np.cos(position_enc[:, 1::2])], axis=-1)


def apply_rope(x, time):
    pos = create_sinusoidal_positions(x.shape[-2], x.shape[-1], time)
    sin, cos = np.split(pos, 2, axis=-1)
    sin_pos = np.stack([sin, sin], axis=-1).reshape(pos.shape)
    cos_pos = np.stack([cos, cos], axis=-1).reshape(pos.shape)
    rotated = np.stack([-x[..., 1::2], x[..., ::2]], axis=-1).reshape(x.shape)
    return x * cos_pos + rotated * sin_pos


def setup_inputs():
    s = mx_kscale(C)
    x = bf(np.random.standard_normal((N, C)) * s)
    w = np.random.standard_normal((2 * C, C)) / np.sqrt(C) / s[None, :]
    words, scales = pack4(np.ascontiguousarray(w.T))
    return {"x": x, "W_qk_words": words, "W_qk_scales": scales}


def reference(x, W_qk_words, W_qk_scales):
    qk = mxq(f64(x), 1, "e5m2") @ unpack4(W_qk_words, W_qk_scales)
    qk = qk.reshape(N, 2, H, D).transpose(1, 2, 0, 3)
    q, k = qk[0], qk[1]
    return apply_rope(q, SIN_TIME), apply_rope(k, SIN_TIME)

@@ -1,0 +1,205 @@
+import math
+from contextlib import ExitStack
+
+import concourse.mybir as mybir
+from concourse.masks import make_identity
+
+FLOPS = 2 * 512 * 2048 * 4096
+
+F32 = mybir.dt.float32
+BF16 = mybir.dt.bfloat16
+I32 = mybir.dt.int32
+U32 = mybir.dt.uint32
+U8 = mybir.dt.uint8
+E5M2X4 = mybir.dt.float8_e5m2_x4
+E2M1X4 = mybir.dt.float4_e2m1fn_x4
+ALU = mybir.AluOpType
+ACT = mybir.ActivationFunctionType
+
+P = 128
+TILES = 4
+PASSES = 4
+BLOCKS = 8
+NB = 512
+PAIRS = 64
+
+
+def theta(e):
+    return 10000.0 ** (-e / 64.0)
+
+
+def tile_attentionblock_pa_kernel(tc, x, w_words, w_scales, q_out, k_out):
+    nc = tc.nc
+    with ExitStack() as ctx:
+        const = ctx.enter_context(tc.tile_pool(name="const", bufs=1))
+        work = ctx.enter_context(tc.tile_pool(name="work", bufs=4))
+        outp = ctx.enter_context(tc.tile_pool(name="outp", bufs=3))
+        psum = ctx.enter_context(tc.psum_pool(name="psum", bufs=8))
+
+        zero = const.tile([P, 1], F32, name="zero")
+        nc.vector.memset(zero[:], 0.0)
+        warm = const.tile([P, 1], F32, name="warm")
+        nc.scalar.activation(out=warm[:], in_=zero[:], func=ACT.Sin)
+
+        plane_a = const.tile([P, PASSES, NB], U8, name="plane_a", align_bytes=64)
+        plane_b = const.tile([P, PASSES, (BLOCKS - 1) * NB], U8, name="plane_b", align_bytes=64)
+        nc.vector.memset(plane_a[:].bitcast(I32), 0)
+
+        ident = const.tile([P, P], F32, name="ident")
+        make_identity(nc, ident[:])
+        pos_i = const.tile([P, TILES], I32, name="pos_i")
+        nc.gpsimd.iota(pos_i[:], pattern=[[1, TILES]], base=0, channel_multiplier=TILES)
+        nc.gpsimd.memset(plane_b[:].bitcast(F32), 0.0)
+
+        x_view = x.rearrange("(p a) k -> p a k", a=TILES)
+        x_sb = []
+        w_sb = []
+        for a in range(TILES):
+            x_sb.append(const.tile([P, 2048], BF16, name="x_sb%d" % a))
+        for j in range(BLOCKS):
+            w_sb.append(const.tile([P, PASSES, 2 * NB], U8, name="w_sb%d" % j, align_bytes=64))
+
+        def load_x(a):
+            nc.sync.dma_start(out=x_sb[a][:], in_=x_view[:, a, :])
+
+        def load_w(j):
+            nc.sync.dma_start(
+                out=w_sb[j][:].bitcast(I32),
+                in_=w_words[:, :, 2 * NB * j : 2 * NB * (j + 1)].rearrange("g p n -> p g n").bitcast(I32),
+            )
+
+        def load_scales(plane, c0, c1):
+            for q in range(4):
+                nc.sync.dma_start(
+                    out=plane[32 * q : 32 * q + 4, :, :].bitcast(I32),
+                    in_=w_scales[:, 4 * q : 4 * q + 4, c0:c1].rearrange("g r n -> r g n").bitcast(I32),
+                )
+
+        load_x(0)
+        load_scales(plane_a, 0, NB)
+        load_w(0)
+        load_x(1)
+        load_x(2)
+        load_x(3)
+        load_w(1)
+        load_scales(plane_b, NB, BLOCKS * NB)
+        for j in range(2, BLOCKS):
+            load_w(j)
+
+        pos_f = const.tile([P, TILES], F32, name="pos_f")
+        nc.vector.tensor_copy(out=pos_f[:], in_=pos_i[:])
+        ang_hi = const.tile([P, TILES, 8], F32, name="ang_hi")
+        for hi in range(8):
+            nc.scalar.activation(out=ang_hi[:, :, hi], in_=pos_f[:], func=ACT.Copy, scale=theta(8 * hi))
+        ang = const.tile([P, 2, TILES, 8, 8], F32, name="ang")
+        for lo in range(8):
+            nc.scalar.activation(out=ang[:, 0, :, :, lo], in_=ang_hi[:], func=ACT.Copy, scale=theta(lo))
+        nc.vector.tensor_scalar(
+            out=ang[:, 1], in0=ang[:, 0], scalar1=math.pi / 2.0, scalar2=None, op0=ALU.add
+        )
+        ang_flat = ang[:].rearrange("p f a h l -> p (f a h l)")
+        turns = const.tile([P, 2 * TILES * PAIRS], I32, name="turns")
+        nc.vector.tensor_scalar(
+            out=turns[:], in0=ang_flat, scalar1=1.0 / math.pi, scalar2=0.25, op0=ALU.mult, op1=ALU.add
+        )
+        red = const.tile([P, 2 * TILES * PAIRS], F32, name="red")
+        nc.vector.scalar_tensor_tensor(
+            out=red[:], in0=turns[:], scalar=-math.pi, in1=ang_flat, op0=ALU.mult, op1=ALU.add
+        )
+        par = const.tile([P, 2 * TILES * PAIRS], I32, name="par")
+        nc.vector.tensor_scalar(out=par[:], in0=turns[:], scalar1=1, scalar2=None, op0=ALU.bitwise_and)
+        sgn = const.tile([P, 2, TILES, PAIRS], F32, name="sgn")
+        nc.vector.tensor_scalar(
+            out=sgn[:].rearrange("p f a i -> p (f a i)"), in0=par[:], scalar1=-2.0, scalar2=1.0,
+            op0=ALU.mult, op1=ALU.add,
+        )
+        raw = const.tile([P, 2, TILES, PAIRS], F32, name="raw")
+        nc.scalar.activation(out=raw[:].rearrange("p f a i -> p (f a i)"), in_=red[:], func=ACT.Sin)
+        ktab = const.tile([P, TILES, 2, PAIRS, 2], F32, name="ktab")
+        nc.vector.tensor_tensor(out=ktab[:, :, 0, :, 0], in0=raw[:, 1], in1=sgn[:, 1], op=ALU.mult)
+        nc.vector.tensor_tensor(out=ktab[:, :, 1, :, 1], in0=raw[:, 1], in1=sgn[:, 1], op=ALU.mult)
+        nc.vector.tensor_tensor(out=ktab[:, :, 0, :, 1], in0=raw[:, 0], in1=sgn[:, 0], op=ALU.mult)
+        nc.vector.scalar_tensor_tensor(
+            out=ktab[:, :, 1, :, 0], in0=raw[:, 0], scalar=-1.0, in1=sgn[:, 0], op0=ALU.mult, op1=ALU.mult
+        )
+
+        grouped = []
+        x_codes = []
+        x_scales = []
+        for a in range(TILES):
+            grouped.append(const.tile([P, PASSES, P, 4], BF16, name="grouped%d" % a, align_bytes=64))
+            x_codes.append(const.tile([P, PASSES * P], U32, name="x_codes%d" % a, align_bytes=64))
+            x_scales.append(const.tile([P, PASSES * P], U8, name="x_scales%d" % a, align_bytes=64))
+
+        def prepare_x(a):
+            words = x_sb[a][:].bitcast(F32)
+            for half in range(2):
+                xt = psum.tile([P, 2, 2, P], F32, tag="bank", name="xt")
+                for g2 in range(2):
+                    g = 2 * half + g2
+                    for u in range(2):
+                        nc.tensor.transpose(xt[:, g2, u, :], words[:, 256 * g + u : 256 * (g + 1) : 2], ident[:])
+                nc.scalar.copy(
+                    out=grouped[a][:, 2 * half : 2 * half + 2].bitcast(F32),
+                    in_=xt[:].rearrange("p g u r -> p g r u"),
+                )
+                nc.vector.quantize_mx(
+                    out=x_codes[a][:, 256 * half : 256 * (half + 1)].bitcast(E5M2X4),
+                    scales=x_scales[a][:, 256 * half : 256 * (half + 1)],
+                    in_=grouped[a][:, 2 * half : 2 * half + 2].rearrange("p g r t -> p (g r t)"),
+                )
+
+        res_tiles = {}
+
+        def block_tile(j, a):
+            acc = psum.tile([P, NB], F32, tag="bank", name="acc")
+            for g in range(PASSES):
+                if j == 0:
+                    scale_ap = plane_a[:, g, :]
+                else:
+                    scale_ap = plane_b[:, g, NB * (j - 1) : NB * j]
+                nc.tensor.matmul_mx(
+                    out=acc[:],
+                    lhsT=x_codes[a][:, P * g : P * (g + 1)].bitcast(E5M2X4),
+                    lhsT_scale=x_scales[a][:, P * g : P * (g + 1)],
+                    rhs=w_sb[j][:, g, :].bitcast(E2M1X4),
+                    rhs_scale=scale_ap,
+                    start=(g == 0),
+                    stop=(g == PASSES - 1),
+                )
+            prod = work.tile([P, 2, 4, PAIRS, 2], F32, name="prod")
+            shape = [P, 2, 4, PAIRS, 2]
+            nc.vector.tensor_tensor(
+                out=prod[:],
+                in0=acc[:].rearrange("p (h i e) -> p e h i", h=4, i=PAIRS, e=2).unsqueeze(4).to_broadcast(shape),
+                in1=ktab[:, a].unsqueeze(2).to_broadcast(shape),
+                op=ALU.mult,
+            )
+            if a == 0:
+                res_tiles[j] = outp.tile([P, 4, TILES, P], F32, name="res")
+            res = res_tiles[j]
+            nc.gpsimd.tensor_tensor(
+                out=res[:, :, a, :],
+                in0=prod[:, 0].rearrange("p h i w -> p h (i w)"),
+                in1=prod[:, 1].rearrange("p h i w -> p h (i w)"),
+                op=ALU.add,
+            )
+            if a == TILES - 1:
+                dst = q_out if j < 4 else k_out
+                h0 = 4 * (j % 4)
+                nc.scalar.dma_start(
+                    out=dst[h0 : h0 + 4].rearrange("h (p a) d -> p h (a d)", a=TILES),
+                    in_=res[:].rearrange("p h a d -> p h (a d)"),
+                )
+
+        prepare_x(0)
+        prepare_x(1)
+        block_tile(0, 0)
+        prepare_x(2)
+        block_tile(0, 1)
+        prepare_x(3)
+        block_tile(0, 2)
+        block_tile(0, 3)
+        for j in range(1, BLOCKS):
+            for a in range(TILES):
+                block_tile(j, a)

@@ -22,6 +22,7 @@ PASSES = 4
 BLOCKS = 8
 NB = 512
 PAIRS = 64
+PLANES = 3
 
 
 def theta(e):
@@ -32,7 +33,8 @@ def tile_attentionblock_pa_kernel(tc, x, w_words, w_scales, q_out, k_out):
     nc = tc.nc
     with ExitStack() as ctx:
         const = ctx.enter_context(tc.tile_pool(name="const", bufs=1))
-        work = ctx.enter_context(tc.tile_pool(name="work", bufs=4))
+        work1 = ctx.enter_context(tc.tile_pool(name="work1", bufs=3))
+        work2 = ctx.enter_context(tc.tile_pool(name="work2", bufs=3))
         outp = ctx.enter_context(tc.tile_pool(name="outp", bufs=3))
         psum = ctx.enter_context(tc.psum_pool(name="psum", bufs=8))
 
@@ -41,15 +43,15 @@ def tile_attentionblock_pa_kernel(tc, x, w_words, w_scales, q_out, k_out):
         warm = const.tile([P, 1], F32, name="warm")
         nc.scalar.activation(out=warm[:], in_=zero[:], func=ACT.Sin)
 
-        plane_a = const.tile([P, PASSES, NB], U8, name="plane_a", align_bytes=64)
-        plane_b = const.tile([P, PASSES, (BLOCKS - 1) * NB], U8, name="plane_b", align_bytes=64)
-        nc.vector.memset(plane_a[:].bitcast(I32), 0)
+        planes = []
+        for s in range(PLANES):
+            planes.append(const.tile([P, PASSES, NB], U8, name="plane%d" % s, align_bytes=64))
+        nc.vector.memset(planes[0][:].bitcast(I32), 0)
 
-        ident = const.tile([P, P], F32, name="ident")
-        make_identity(nc, ident[:])
         pos_i = const.tile([P, TILES], I32, name="pos_i")
         nc.gpsimd.iota(pos_i[:], pattern=[[1, TILES]], base=0, channel_multiplier=TILES)
-        nc.gpsimd.memset(plane_b[:].bitcast(F32), 0.0)
+        ident = const.tile([P, P], F32, name="ident")
+        make_identity(nc, ident[:])
 
         x_view = x.rearrange("(p a) k -> p a k", a=TILES)
         x_sb = []
@@ -59,8 +61,8 @@ def tile_attentionblock_pa_kernel(tc, x, w_words, w_scales, q_out, k_out):
         for j in range(BLOCKS):
             w_sb.append(const.tile([P, PASSES, 2 * NB], U8, name="w_sb%d" % j, align_bytes=64))
 
-        def load_x(a):
-            nc.sync.dma_start(out=x_sb[a][:], in_=x_view[:, a, :])
+        def load_x(a, c0, c1):
+            nc.sync.dma_start(out=x_sb[a][:, c0:c1], in_=x_view[:, a, c0:c1])
 
         def load_w(j):
             nc.sync.dma_start(
@@ -68,60 +70,70 @@ def tile_attentionblock_pa_kernel(tc, x, w_words, w_scales, q_out, k_out):
                 in_=w_words[:, :, 2 * NB * j : 2 * NB * (j + 1)].rearrange("g p n -> p g n").bitcast(I32),
             )
 
-        def load_scales(plane, c0, c1):
+        def load_scales(j):
             for q in range(4):
                 nc.sync.dma_start(
-                    out=plane[32 * q : 32 * q + 4, :, :].bitcast(I32),
-                    in_=w_scales[:, 4 * q : 4 * q + 4, c0:c1].rearrange("g r n -> r g n").bitcast(I32),
+                    out=planes[j % PLANES][32 * q : 32 * q + 4, :, :].bitcast(I32),
+                    in_=w_scales[:, 4 * q : 4 * q + 4, NB * j : NB * (j + 1)].rearrange("g r n -> r g n").bitcast(I32),
                 )
 
-        load_x(0)
-        load_scales(plane_a, 0, NB)
+        load_x(0, 0, 1024)
+        load_x(0, 1024, 2048)
+        load_scales(0)
         load_w(0)
-        load_x(1)
-        load_x(2)
-        load_x(3)
-        load_w(1)
-        load_scales(plane_b, NB, BLOCKS * NB)
-        for j in range(2, BLOCKS):
-            load_w(j)
+        load_x(1, 0, 2048)
 
         pos_f = const.tile([P, TILES], F32, name="pos_f")
         nc.vector.tensor_copy(out=pos_f[:], in_=pos_i[:])
         ang_hi = const.tile([P, TILES, 8], F32, name="ang_hi")
         for hi in range(8):
-            nc.scalar.activation(out=ang_hi[:, :, hi], in_=pos_f[:], func=ACT.Copy, scale=theta(8 * hi))
+            nc.vector.tensor_scalar(
+                out=ang_hi[:, :, hi], in0=pos_f[:], scalar1=theta(8 * hi), scalar2=None, op0=ALU.mult
+            )
         ang = const.tile([P, 2, TILES, 8, 8], F32, name="ang")
         for lo in range(8):
-            nc.scalar.activation(out=ang[:, 0, :, :, lo], in_=ang_hi[:], func=ACT.Copy, scale=theta(lo))
+            nc.vector.tensor_scalar(
+                out=ang[:, 1, :, :, lo], in0=ang_hi[:], scalar1=theta(lo), scalar2=None, op0=ALU.mult
+            )
         nc.vector.tensor_scalar(
-            out=ang[:, 1], in0=ang[:, 0], scalar1=math.pi / 2.0, scalar2=None, op0=ALU.add
+            out=ang[:, 0], in0=ang[:, 1], scalar1=math.pi / 2.0, scalar2=None, op0=ALU.add
         )
         ang_flat = ang[:].rearrange("p f a h l -> p (f a h l)")
-        turns = const.tile([P, 2 * TILES * PAIRS], I32, name="turns")
+        half_w = TILES * PAIRS
+        turns = const.tile([P, 2 * half_w], I32, name="turns")
         nc.vector.tensor_scalar(
             out=turns[:], in0=ang_flat, scalar1=1.0 / math.pi, scalar2=0.25, op0=ALU.mult, op1=ALU.add
         )
-        red = const.tile([P, 2 * TILES * PAIRS], F32, name="red")
+        red = const.tile([P, 2 * half_w], F32, name="red")
         nc.vector.scalar_tensor_tensor(
             out=red[:], in0=turns[:], scalar=-math.pi, in1=ang_flat, op0=ALU.mult, op1=ALU.add
         )
-        par = const.tile([P, 2 * TILES * PAIRS], I32, name="par")
+        raw3 = const.tile([P, 3, TILES, PAIRS], F32, name="raw3")
+        sgn3 = const.tile([P, 3, TILES, PAIRS], F32, name="sgn3")
+        nc.scalar.activation(out=raw3[:, 1:3].rearrange("p f a i -> p (f a i)"), in_=red[:], func=ACT.Sin)
+        nc.scalar.activation(
+            out=raw3[:, 0].rearrange("p a i -> p (a i)"), in_=red[:, half_w : 2 * half_w], func=ACT.Sin
+        )
+        par = const.tile([P, 2 * half_w], I32, name="par")
         nc.vector.tensor_scalar(out=par[:], in0=turns[:], scalar1=1, scalar2=None, op0=ALU.bitwise_and)
-        sgn = const.tile([P, 2, TILES, PAIRS], F32, name="sgn")
         nc.vector.tensor_scalar(
-            out=sgn[:].rearrange("p f a i -> p (f a i)"), in0=par[:], scalar1=-2.0, scalar2=1.0,
+            out=sgn3[:, 1:3].rearrange("p f a i -> p (f a i)"), in0=par[:], scalar1=-2.0, scalar2=1.0,
             op0=ALU.mult, op1=ALU.add,
         )
-        raw = const.tile([P, 2, TILES, PAIRS], F32, name="raw")
-        nc.scalar.activation(out=raw[:].rearrange("p f a i -> p (f a i)"), in_=red[:], func=ACT.Sin)
-        ktab = const.tile([P, TILES, 2, PAIRS, 2], F32, name="ktab")
-        nc.vector.tensor_tensor(out=ktab[:, :, 0, :, 0], in0=raw[:, 1], in1=sgn[:, 1], op=ALU.mult)
-        nc.vector.tensor_tensor(out=ktab[:, :, 1, :, 1], in0=raw[:, 1], in1=sgn[:, 1], op=ALU.mult)
-        nc.vector.tensor_tensor(out=ktab[:, :, 0, :, 1], in0=raw[:, 0], in1=sgn[:, 0], op=ALU.mult)
-        nc.vector.scalar_tensor_tensor(
-            out=ktab[:, :, 1, :, 0], in0=raw[:, 0], scalar=-1.0, in1=sgn[:, 0], op0=ALU.mult, op1=ALU.mult
+        nc.vector.tensor_scalar(
+            out=sgn3[:, 0].rearrange("p a i -> p (a i)"), in0=par[:, half_w : 2 * half_w], scalar1=2.0,
+            scalar2=-1.0, op0=ALU.mult, op1=ALU.add,
         )
+        nc.vector.memset(planes[1][:].bitcast(I32), 0)
+        nc.vector.memset(planes[2][:].bitcast(I32), 0)
+
+        load_scales(1)
+        load_w(1)
+        load_x(2, 0, 2048)
+        load_x(3, 0, 2048)
+        load_scales(2)
+        for j in range(2, BLOCKS):
+            load_w(j)
 
         grouped = []
         x_codes = []
@@ -149,57 +161,106 @@ def tile_attentionblock_pa_kernel(tc, x, w_words, w_scales, q_out, k_out):
                     in_=grouped[a][:, 2 * half : 2 * half + 2].rearrange("p g r t -> p (g r t)"),
                 )
 
-        res_tiles = {}
+        ktab = const.tile([P, TILES, 2, PAIRS, 2], F32, name="ktab")
 
-        def block_tile(j, a):
+        def finish_table():
+            for e in range(2):
+                nc.vector.tensor_tensor(
+                    out=ktab[:, :, e, :, :],
+                    in0=raw3[:, 1 - e : 3 - e].rearrange("p w a i -> p a i w"),
+                    in1=sgn3[:, 1 - e : 3 - e].rearrange("p w a i -> p a i w"),
+                    op=ALU.mult,
+                )
+
+        res_tiles = {}
+        prod_tiles = {}
+        shape = [P, 2, 4, PAIRS, 2]
+
+        def matmuls(j, a):
             acc = psum.tile([P, NB], F32, tag="bank", name="acc")
             for g in range(PASSES):
-                if j == 0:
-                    scale_ap = plane_a[:, g, :]
-                else:
-                    scale_ap = plane_b[:, g, NB * (j - 1) : NB * j]
                 nc.tensor.matmul_mx(
                     out=acc[:],
                     lhsT=x_codes[a][:, P * g : P * (g + 1)].bitcast(E5M2X4),
                     lhsT_scale=x_scales[a][:, P * g : P * (g + 1)],
                     rhs=w_sb[j][:, g, :].bitcast(E2M1X4),
-                    rhs_scale=scale_ap,
+                    rhs_scale=planes[j % PLANES][:, g, :],
                     start=(g == 0),
                     stop=(g == PASSES - 1),
                 )
-            prod = work.tile([P, 2, 4, PAIRS, 2], F32, name="prod")
-            shape = [P, 2, 4, PAIRS, 2]
+            return acc
+
+        def product(acc, a, out_ap):
             nc.vector.tensor_tensor(
-                out=prod[:],
+                out=out_ap,
                 in0=acc[:].rearrange("p (h i e) -> p e h i", h=4, i=PAIRS, e=2).unsqueeze(4).to_broadcast(shape),
                 in1=ktab[:, a].unsqueeze(2).to_broadcast(shape),
                 op=ALU.mult,
             )
-            if a == 0:
+
+        def store(j, a0, a1):
+            dst = q_out if j < 4 else k_out
+            h0 = 4 * (j % 4)
+            nc.scalar.dma_start(
+                out=dst[h0 : h0 + 4].rearrange("h (p a) d -> p h a d", a=TILES)[:, :, a0:a1, :],
+                in_=res_tiles[j][:, :, a0:a1, :],
+            )
+
+        def single(j, a, engine):
+            acc = matmuls(j, a)
+            if j not in res_tiles:
                 res_tiles[j] = outp.tile([P, 4, TILES, P], F32, name="res")
-            res = res_tiles[j]
-            nc.gpsimd.tensor_tensor(
-                out=res[:, :, a, :],
+            prod = work1.tile(shape, F32, name="prod1")
+            product(acc, a, prod[:])
+            engine.tensor_tensor(
+                out=res_tiles[j][:, :, a, :],
                 in0=prod[:, 0].rearrange("p h i w -> p h (i w)"),
                 in1=prod[:, 1].rearrange("p h i w -> p h (i w)"),
                 op=ALU.add,
             )
-            if a == TILES - 1:
-                dst = q_out if j < 4 else k_out
-                h0 = 4 * (j % 4)
-                nc.scalar.dma_start(
-                    out=dst[h0 : h0 + 4].rearrange("h (p a) d -> p h (a d)", a=TILES),
-                    in_=res[:].rearrange("p h a d -> p h (a d)"),
-                )
+
+        def double(j, a0):
+            if j not in res_tiles:
+                res_tiles[j] = outp.tile([P, 4, TILES, P], F32, name="res")
+            prod = work2.tile([P, 2] + shape[1:], F32, name="prod2")
+            for t in range(2):
+                acc = matmuls(j, a0 + t)
+                product(acc, a0 + t, prod[:, t])
+            nc.gpsimd.tensor_tensor(
+                out=res_tiles[j][:, :, a0 : a0 + 2, :].rearrange("p h t d -> p t h d"),
+                in0=prod[:, :, 0].rearrange("p t h i w -> p t h (i w)"),
+                in1=prod[:, :, 1].rearrange("p t h i w -> p t h (i w)"),
+                op=ALU.add,
+            )
 
         prepare_x(0)
+        finish_table()
+        single(0, 0, nc.gpsimd)
         prepare_x(1)
-        block_tile(0, 0)
+        single(1, 0, nc.gpsimd)
+        single(0, 1, nc.gpsimd)
         prepare_x(2)
-        block_tile(0, 1)
+        single(1, 1, nc.gpsimd)
+        single(0, 2, nc.gpsimd)
         prepare_x(3)
-        block_tile(0, 2)
-        block_tile(0, 3)
-        for j in range(1, BLOCKS):
-            for a in range(TILES):
-                block_tile(j, a)
+        single(1, 2, nc.gpsimd)
+        single(0, 3, nc.gpsimd)
+        store(0, 0, TILES)
+        load_scales(3)
+        single(1, 3, nc.gpsimd)
+        store(1, 0, TILES)
+        load_scales(4)
+        for j in range(2, BLOCKS - 1):
+            double(j, 0)
+            double(j, 2)
+            store(j, 0, TILES)
+            if j + PLANES < BLOCKS:
+                load_scales(j + PLANES)
+        j = BLOCKS - 1
+        single(j, 0, nc.gpsimd)
+        single(j, 1, nc.gpsimd)
+        store(j, 0, 2)
+        single(j, 2, nc.gpsimd)
+        store(j, 2, 3)
+        single(j, 3, nc.vector)
+        store(j, 3, 4)

@@ -22,7 +22,6 @@ PASSES = 4
 BLOCKS = 8
 NB = 512
 PAIRS = 64
-PLANES = 3
 
 
 def theta(e):
@@ -33,25 +32,25 @@ def tile_attentionblock_pa_kernel(tc, x, w_words, w_scales, q_out, k_out):
     nc = tc.nc
     with ExitStack() as ctx:
         const = ctx.enter_context(tc.tile_pool(name="const", bufs=1))
-        work1 = ctx.enter_context(tc.tile_pool(name="work1", bufs=3))
+        work1 = ctx.enter_context(tc.tile_pool(name="work1", bufs=6))
         work2 = ctx.enter_context(tc.tile_pool(name="work2", bufs=3))
         outp = ctx.enter_context(tc.tile_pool(name="outp", bufs=3))
         psum = ctx.enter_context(tc.psum_pool(name="psum", bufs=8))
 
-        zero = const.tile([P, 1], F32, name="zero")
-        nc.vector.memset(zero[:], 0.0)
-        warm = const.tile([P, 1], F32, name="warm")
-        nc.scalar.activation(out=warm[:], in_=zero[:], func=ACT.Sin)
-
         planes = []
-        for s in range(PLANES):
-            planes.append(const.tile([P, PASSES, NB], U8, name="plane%d" % s, align_bytes=64))
+        for j in range(BLOCKS):
+            planes.append(const.tile([P, PASSES, NB], U8, name="plane%d" % j, align_bytes=64))
         nc.vector.memset(planes[0][:].bitcast(I32), 0)
 
         pos_i = const.tile([P, TILES], I32, name="pos_i")
         nc.gpsimd.iota(pos_i[:], pattern=[[1, TILES]], base=0, channel_multiplier=TILES)
+        zero = const.tile([P, 1], F32, name="zero")
+        nc.gpsimd.memset(zero[:], 0.0)
+        warm = const.tile([P, 1], F32, name="warm")
+        nc.scalar.activation(out=warm[:], in_=zero[:], func=ACT.Sin)
         ident = const.tile([P, P], F32, name="ident")
         make_identity(nc, ident[:])
+        nc.gpsimd.memset(planes[2][:].bitcast(F32), 0.0)
 
         x_view = x.rearrange("(p a) k -> p a k", a=TILES)
         x_sb = []
@@ -64,42 +63,45 @@ def tile_attentionblock_pa_kernel(tc, x, w_words, w_scales, q_out, k_out):
         def load_x(a, c0, c1):
             nc.sync.dma_start(out=x_sb[a][:, c0:c1], in_=x_view[:, a, c0:c1])
 
-        def load_w(j):
+        def load_w(j, g0, g1):
             nc.sync.dma_start(
-                out=w_sb[j][:].bitcast(I32),
-                in_=w_words[:, :, 2 * NB * j : 2 * NB * (j + 1)].rearrange("g p n -> p g n").bitcast(I32),
+                out=w_sb[j][:, g0:g1, :].bitcast(I32),
+                in_=w_words[g0:g1, :, 2 * NB * j : 2 * NB * (j + 1)].rearrange("g p n -> p g n").bitcast(I32),
+            )
+
+        def load_filler(j):
+            nc.sync.dma_start(
+                out=planes[j][:].rearrange("p g n -> p (g n)").bitcast(I32),
+                in_=w_scales.rearrange("g q (s n) -> (g q s) n", s=2).bitcast(I32),
             )
 
         def load_scales(j):
             for q in range(4):
                 nc.sync.dma_start(
-                    out=planes[j % PLANES][32 * q : 32 * q + 4, :, :].bitcast(I32),
+                    out=planes[j][32 * q : 32 * q + 4, :, :].bitcast(I32),
                     in_=w_scales[:, 4 * q : 4 * q + 4, NB * j : NB * (j + 1)].rearrange("g r n -> r g n").bitcast(I32),
                 )
 
         load_x(0, 0, 1024)
         load_x(0, 1024, 2048)
         load_scales(0)
-        load_w(0)
+        load_w(0, 0, 2)
+        load_w(0, 2, 4)
         load_x(1, 0, 2048)
 
-        pos_f = const.tile([P, TILES], F32, name="pos_f")
-        nc.vector.tensor_copy(out=pos_f[:], in_=pos_i[:])
-        ang_hi = const.tile([P, TILES, 8], F32, name="ang_hi")
-        for hi in range(8):
+        half_w = TILES * PAIRS
+        ang = const.tile([P, 2, TILES, PAIRS], F32, name="ang")
+        nc.vector.tensor_copy(out=ang[:, 1, :, 0], in_=pos_i[:])
+        for b in range(6):
+            w = 2 ** b
             nc.vector.tensor_scalar(
-                out=ang_hi[:, :, hi], in0=pos_f[:], scalar1=theta(8 * hi), scalar2=None, op0=ALU.mult
+                out=ang[:, 1, :, w : 2 * w], in0=ang[:, 1, :, 0:w], scalar1=theta(w), scalar2=None, op0=ALU.mult
             )
-        ang = const.tile([P, 2, TILES, 8, 8], F32, name="ang")
-        for lo in range(8):
-            nc.vector.tensor_scalar(
-                out=ang[:, 1, :, :, lo], in0=ang_hi[:], scalar1=theta(lo), scalar2=None, op0=ALU.mult
-            )
+        nc.vector.memset(planes[1][:].bitcast(I32), 0)
         nc.vector.tensor_scalar(
             out=ang[:, 0], in0=ang[:, 1], scalar1=math.pi / 2.0, scalar2=None, op0=ALU.add
         )
-        ang_flat = ang[:].rearrange("p f a h l -> p (f a h l)")
-        half_w = TILES * PAIRS
+        ang_flat = ang[:].rearrange("p f a i -> p (f a i)")
         turns = const.tile([P, 2 * half_w], I32, name="turns")
         nc.vector.tensor_scalar(
             out=turns[:], in0=ang_flat, scalar1=1.0 / math.pi, scalar2=0.25, op0=ALU.mult, op1=ALU.add
@@ -124,16 +126,25 @@ def tile_attentionblock_pa_kernel(tc, x, w_words, w_scales, q_out, k_out):
             out=sgn3[:, 0].rearrange("p a i -> p (a i)"), in0=par[:, half_w : 2 * half_w], scalar1=2.0,
             scalar2=-1.0, op0=ALU.mult, op1=ALU.add,
         )
-        nc.vector.memset(planes[1][:].bitcast(I32), 0)
-        nc.vector.memset(planes[2][:].bitcast(I32), 0)
 
         load_scales(1)
-        load_w(1)
+        load_w(1, 0, 4)
         load_x(2, 0, 2048)
         load_x(3, 0, 2048)
         load_scales(2)
-        for j in range(2, BLOCKS):
-            load_w(j)
+        load_w(2, 0, 4)
+        for j in range(3, BLOCKS):
+            load_filler(j)
+        load_w(3, 0, 4)
+        load_w(4, 0, 4)
+        load_w(5, 0, 4)
+        load_scales(3)
+        load_scales(4)
+        load_w(6, 0, 4)
+        load_scales(5)
+        load_w(7, 0, 4)
+        load_scales(6)
+        load_scales(7)
 
         grouped = []
         x_codes = []
@@ -143,37 +154,42 @@ def tile_attentionblock_pa_kernel(tc, x, w_words, w_scales, q_out, k_out):
             x_codes.append(const.tile([P, PASSES * P], U32, name="x_codes%d" % a, align_bytes=64))
             x_scales.append(const.tile([P, PASSES * P], U8, name="x_scales%d" % a, align_bytes=64))
 
-        def prepare_x(a):
+        def quantise(a, g0, g1):
+            nc.vector.quantize_mx(
+                out=x_codes[a][:, P * g0 : P * g1].bitcast(E5M2X4),
+                scales=x_scales[a][:, P * g0 : P * g1],
+                in_=grouped[a][:, g0:g1].rearrange("p g r t -> p (g r t)"),
+            )
+
+        def turn_x(a, half):
             words = x_sb[a][:].bitcast(F32)
-            for half in range(2):
-                xt = psum.tile([P, 2, 2, P], F32, tag="bank", name="xt")
-                for g2 in range(2):
-                    g = 2 * half + g2
-                    for u in range(2):
-                        nc.tensor.transpose(xt[:, g2, u, :], words[:, 256 * g + u : 256 * (g + 1) : 2], ident[:])
-                nc.scalar.copy(
-                    out=grouped[a][:, 2 * half : 2 * half + 2].bitcast(F32),
-                    in_=xt[:].rearrange("p g u r -> p g r u"),
-                )
-                nc.vector.quantize_mx(
-                    out=x_codes[a][:, 256 * half : 256 * (half + 1)].bitcast(E5M2X4),
-                    scales=x_scales[a][:, 256 * half : 256 * (half + 1)],
-                    in_=grouped[a][:, 2 * half : 2 * half + 2].rearrange("p g r t -> p (g r t)"),
-                )
+            xt = psum.tile([P, 2, 2, P], F32, tag="bank", name="xt")
+            for g2 in range(2):
+                g = 2 * half + g2
+                for u in range(2):
+                    nc.tensor.transpose(xt[:, g2, u, :], words[:, 256 * g + u : 256 * (g + 1) : 2], ident[:])
+            nc.scalar.copy(
+                out=grouped[a][:, 2 * half : 2 * half + 2].bitcast(F32),
+                in_=xt[:].rearrange("p g u r -> p g r u"),
+            )
+
+        def prepare_x(a):
+            turn_x(a, 0)
+            turn_x(a, 1)
+            quantise(a, 0, PASSES)
 
         ktab = const.tile([P, TILES, 2, PAIRS, 2], F32, name="ktab")
 
-        def finish_table():
+        def finish_table(engine, a0, a1):
             for e in range(2):
-                nc.vector.tensor_tensor(
-                    out=ktab[:, :, e, :, :],
-                    in0=raw3[:, 1 - e : 3 - e].rearrange("p w a i -> p a i w"),
-                    in1=sgn3[:, 1 - e : 3 - e].rearrange("p w a i -> p a i w"),
+                engine.tensor_tensor(
+                    out=ktab[:, a0:a1, e, :, :],
+                    in0=raw3[:, 1 - e : 3 - e, a0:a1].rearrange("p w a i -> p a i w"),
+                    in1=sgn3[:, 1 - e : 3 - e, a0:a1].rearrange("p w a i -> p a i w"),
                     op=ALU.mult,
                 )
 
         res_tiles = {}
-        prod_tiles = {}
         shape = [P, 2, 4, PAIRS, 2]
 
         def matmuls(j, a):
@@ -184,7 +200,7 @@ def tile_attentionblock_pa_kernel(tc, x, w_words, w_scales, q_out, k_out):
                     lhsT=x_codes[a][:, P * g : P * (g + 1)].bitcast(E5M2X4),
                     lhsT_scale=x_scales[a][:, P * g : P * (g + 1)],
                     rhs=w_sb[j][:, g, :].bitcast(E2M1X4),
-                    rhs_scale=planes[j % PLANES][:, g, :],
+                    rhs_scale=planes[j][:, g, :],
                     start=(g == 0),
                     stop=(g == PASSES - 1),
                 )
@@ -198,26 +214,39 @@ def tile_attentionblock_pa_kernel(tc, x, w_words, w_scales, q_out, k_out):
                 op=ALU.mult,
             )
 
-        def store(j, a0, a1):
+        def out_view(j):
             dst = q_out if j < 4 else k_out
             h0 = 4 * (j % 4)
-            nc.scalar.dma_start(
-                out=dst[h0 : h0 + 4].rearrange("h (p a) d -> p h a d", a=TILES)[:, :, a0:a1, :],
-                in_=res_tiles[j][:, :, a0:a1, :],
-            )
+            return dst[h0 : h0 + 4].rearrange("h (p a) d -> p h a d", a=TILES)
 
-        def single(j, a, engine):
+        def store(j):
+            nc.scalar.dma_start(out=out_view(j), in_=res_tiles[j][:])
+
+        def single(j, a):
             acc = matmuls(j, a)
             if j not in res_tiles:
                 res_tiles[j] = outp.tile([P, 4, TILES, P], F32, name="res")
             prod = work1.tile(shape, F32, name="prod1")
             product(acc, a, prod[:])
-            engine.tensor_tensor(
+            nc.gpsimd.tensor_tensor(
                 out=res_tiles[j][:, :, a, :],
                 in0=prod[:, 0].rearrange("p h i w -> p h (i w)"),
                 in1=prod[:, 1].rearrange("p h i w -> p h (i w)"),
                 op=ALU.add,
             )
+
+        def lone(j, a, engine):
+            acc = matmuls(j, a)
+            prod = work1.tile(shape, F32, name="prod1")
+            product(acc, a, prod[:])
+            part = const.tile([P, 4, P], F32, name="part%d" % a)
+            engine.tensor_tensor(
+                out=part[:],
+                in0=prod[:, 0].rearrange("p h i w -> p h (i w)"),
+                in1=prod[:, 1].rearrange("p h i w -> p h (i w)"),
+                op=ALU.add,
+            )
+            nc.scalar.dma_start(out=out_view(j)[:, :, a, :], in_=part[:])
 
         def double(j, a0):
             if j not in res_tiles:
@@ -233,34 +262,30 @@ def tile_attentionblock_pa_kernel(tc, x, w_words, w_scales, q_out, k_out):
                 op=ALU.add,
             )
 
-        prepare_x(0)
-        finish_table()
-        single(0, 0, nc.gpsimd)
+        finish_table(nc.vector, 0, 1)
+        finish_table(nc.gpsimd, 1, TILES)
+        turn_x(0, 0)
+        quantise(0, 0, 2)
+        turn_x(0, 1)
+        quantise(0, 2, 4)
+        single(0, 0)
         prepare_x(1)
-        single(1, 0, nc.gpsimd)
-        single(0, 1, nc.gpsimd)
+        single(1, 0)
+        single(0, 1)
         prepare_x(2)
-        single(1, 1, nc.gpsimd)
-        single(0, 2, nc.gpsimd)
+        single(1, 1)
+        single(0, 2)
         prepare_x(3)
-        single(1, 2, nc.gpsimd)
-        single(0, 3, nc.gpsimd)
-        store(0, 0, TILES)
-        load_scales(3)
-        single(1, 3, nc.gpsimd)
-        store(1, 0, TILES)
-        load_scales(4)
+        single(1, 2)
+        single(0, 3)
+        store(0)
+        single(1, 3)
+        store(1)
         for j in range(2, BLOCKS - 1):
             double(j, 0)
             double(j, 2)
-            store(j, 0, TILES)
-            if j + PLANES < BLOCKS:
-                load_scales(j + PLANES)
-        j = BLOCKS - 1
-        single(j, 0, nc.gpsimd)
-        single(j, 1, nc.gpsimd)
-        store(j, 0, 2)
-        single(j, 2, nc.gpsimd)
-        store(j, 2, 3)
-        single(j, 3, nc.vector)
-        store(j, 3, 4)
+            store(j)
+        lone(BLOCKS - 1, 0, nc.gpsimd)
+        lone(BLOCKS - 1, 1, nc.gpsimd)
+        lone(BLOCKS - 1, 2, nc.vector)
+        lone(BLOCKS - 1, 3, nc.vector)

@@ -22,6 +22,7 @@ PASSES = 4
 BLOCKS = 8
 NB = 512
 PAIRS = 64
+PLANES = 3
 
 
 def theta(e):
@@ -37,20 +38,20 @@ def tile_attentionblock_pa_kernel(tc, x, w_words, w_scales, q_out, k_out):
         outp = ctx.enter_context(tc.tile_pool(name="outp", bufs=3))
         psum = ctx.enter_context(tc.psum_pool(name="psum", bufs=8))
 
+        zero = const.tile([P, 1], F32, name="zero")
+        nc.vector.memset(zero[:], 0.0)
+        warm = const.tile([P, 1], F32, name="warm")
+        nc.scalar.activation(out=warm[:], in_=zero[:], func=ACT.Sin)
+
         planes = []
-        for j in range(BLOCKS):
-            planes.append(const.tile([P, PASSES, NB], U8, name="plane%d" % j, align_bytes=64))
+        for s in range(PLANES):
+            planes.append(const.tile([P, PASSES, NB], U8, name="plane%d" % s, align_bytes=64))
         nc.vector.memset(planes[0][:].bitcast(I32), 0)
 
         pos_i = const.tile([P, TILES], I32, name="pos_i")
         nc.gpsimd.iota(pos_i[:], pattern=[[1, TILES]], base=0, channel_multiplier=TILES)
-        zero = const.tile([P, 1], F32, name="zero")
-        nc.gpsimd.memset(zero[:], 0.0)
-        warm = const.tile([P, 1], F32, name="warm")
-        nc.scalar.activation(out=warm[:], in_=zero[:], func=ACT.Sin)
         ident = const.tile([P, P], F32, name="ident")
         make_identity(nc, ident[:])
-        nc.gpsimd.memset(planes[2][:].bitcast(F32), 0.0)
 
         x_view = x.rearrange("(p a) k -> p a k", a=TILES)
         x_sb = []
@@ -63,45 +64,42 @@ def tile_attentionblock_pa_kernel(tc, x, w_words, w_scales, q_out, k_out):
         def load_x(a, c0, c1):
             nc.sync.dma_start(out=x_sb[a][:, c0:c1], in_=x_view[:, a, c0:c1])
 
-        def load_w(j, g0, g1):
+        def load_w(j):
             nc.sync.dma_start(
-                out=w_sb[j][:, g0:g1, :].bitcast(I32),
-                in_=w_words[g0:g1, :, 2 * NB * j : 2 * NB * (j + 1)].rearrange("g p n -> p g n").bitcast(I32),
-            )
-
-        def load_filler(j):
-            nc.sync.dma_start(
-                out=planes[j][:].rearrange("p g n -> p (g n)").bitcast(I32),
-                in_=w_scales.rearrange("g q (s n) -> (g q s) n", s=2).bitcast(I32),
+                out=w_sb[j][:].bitcast(I32),
+                in_=w_words[:, :, 2 * NB * j : 2 * NB * (j + 1)].rearrange("g p n -> p g n").bitcast(I32),
             )
 
         def load_scales(j):
             for q in range(4):
                 nc.sync.dma_start(
-                    out=planes[j][32 * q : 32 * q + 4, :, :].bitcast(I32),
+                    out=planes[j % PLANES][32 * q : 32 * q + 4, :, :].bitcast(I32),
                     in_=w_scales[:, 4 * q : 4 * q + 4, NB * j : NB * (j + 1)].rearrange("g r n -> r g n").bitcast(I32),
                 )
 
         load_x(0, 0, 1024)
         load_x(0, 1024, 2048)
         load_scales(0)
-        load_w(0, 0, 2)
-        load_w(0, 2, 4)
+        load_w(0)
         load_x(1, 0, 2048)
 
-        half_w = TILES * PAIRS
-        ang = const.tile([P, 2, TILES, PAIRS], F32, name="ang")
-        nc.vector.tensor_copy(out=ang[:, 1, :, 0], in_=pos_i[:])
-        for b in range(6):
-            w = 2 ** b
+        pos_f = const.tile([P, TILES], F32, name="pos_f")
+        nc.vector.tensor_copy(out=pos_f[:], in_=pos_i[:])
+        ang_hi = const.tile([P, TILES, 8], F32, name="ang_hi")
+        for hi in range(8):
             nc.vector.tensor_scalar(
-                out=ang[:, 1, :, w : 2 * w], in0=ang[:, 1, :, 0:w], scalar1=theta(w), scalar2=None, op0=ALU.mult
+                out=ang_hi[:, :, hi], in0=pos_f[:], scalar1=theta(8 * hi), scalar2=None, op0=ALU.mult
             )
-        nc.vector.memset(planes[1][:].bitcast(I32), 0)
+        ang = const.tile([P, 2, TILES, 8, 8], F32, name="ang")
+        for lo in range(8):
+            nc.vector.tensor_scalar(
+                out=ang[:, 1, :, :, lo], in0=ang_hi[:], scalar1=theta(lo), scalar2=None, op0=ALU.mult
+            )
         nc.vector.tensor_scalar(
             out=ang[:, 0], in0=ang[:, 1], scalar1=math.pi / 2.0, scalar2=None, op0=ALU.add
         )
-        ang_flat = ang[:].rearrange("p f a i -> p (f a i)")
+        ang_flat = ang[:].rearrange("p f a h l -> p (f a h l)")
+        half_w = TILES * PAIRS
         turns = const.tile([P, 2 * half_w], I32, name="turns")
         nc.vector.tensor_scalar(
             out=turns[:], in0=ang_flat, scalar1=1.0 / math.pi, scalar2=0.25, op0=ALU.mult, op1=ALU.add
@@ -126,25 +124,16 @@ def tile_attentionblock_pa_kernel(tc, x, w_words, w_scales, q_out, k_out):
             out=sgn3[:, 0].rearrange("p a i -> p (a i)"), in0=par[:, half_w : 2 * half_w], scalar1=2.0,
             scalar2=-1.0, op0=ALU.mult, op1=ALU.add,
         )
+        nc.vector.memset(planes[1][:].bitcast(I32), 0)
+        nc.vector.memset(planes[2][:].bitcast(I32), 0)
 
         load_scales(1)
-        load_w(1, 0, 4)
+        load_w(1)
         load_x(2, 0, 2048)
         load_x(3, 0, 2048)
         load_scales(2)
-        load_w(2, 0, 4)
-        for j in range(3, BLOCKS):
-            load_filler(j)
-        load_w(3, 0, 4)
-        load_w(4, 0, 4)
-        load_w(5, 0, 4)
-        load_scales(3)
-        load_scales(4)
-        load_w(6, 0, 4)
-        load_scales(5)
-        load_w(7, 0, 4)
-        load_scales(6)
-        load_scales(7)
+        for j in range(2, BLOCKS):
+            load_w(j)
 
         grouped = []
         x_codes = []
@@ -154,42 +143,37 @@ def tile_attentionblock_pa_kernel(tc, x, w_words, w_scales, q_out, k_out):
             x_codes.append(const.tile([P, PASSES * P], U32, name="x_codes%d" % a, align_bytes=64))
             x_scales.append(const.tile([P, PASSES * P], U8, name="x_scales%d" % a, align_bytes=64))
 
-        def quantise(a, g0, g1):
-            nc.vector.quantize_mx(
-                out=x_codes[a][:, P * g0 : P * g1].bitcast(E5M2X4),
-                scales=x_scales[a][:, P * g0 : P * g1],
-                in_=grouped[a][:, g0:g1].rearrange("p g r t -> p (g r t)"),
-            )
-
-        def turn_x(a, half):
-            words = x_sb[a][:].bitcast(F32)
-            xt = psum.tile([P, 2, 2, P], F32, tag="bank", name="xt")
-            for g2 in range(2):
-                g = 2 * half + g2
-                for u in range(2):
-                    nc.tensor.transpose(xt[:, g2, u, :], words[:, 256 * g + u : 256 * (g + 1) : 2], ident[:])
-            nc.scalar.copy(
-                out=grouped[a][:, 2 * half : 2 * half + 2].bitcast(F32),
-                in_=xt[:].rearrange("p g u r -> p g r u"),
-            )
-
         def prepare_x(a):
-            turn_x(a, 0)
-            turn_x(a, 1)
-            quantise(a, 0, PASSES)
+            words = x_sb[a][:].bitcast(F32)
+            for half in range(2):
+                xt = psum.tile([P, 2, 2, P], F32, tag="bank", name="xt")
+                for g2 in range(2):
+                    g = 2 * half + g2
+                    for u in range(2):
+                        nc.tensor.transpose(xt[:, g2, u, :], words[:, 256 * g + u : 256 * (g + 1) : 2], ident[:])
+                nc.scalar.copy(
+                    out=grouped[a][:, 2 * half : 2 * half + 2].bitcast(F32),
+                    in_=xt[:].rearrange("p g u r -> p g r u"),
+                )
+                nc.vector.quantize_mx(
+                    out=x_codes[a][:, 256 * half : 256 * (half + 1)].bitcast(E5M2X4),
+                    scales=x_scales[a][:, 256 * half : 256 * (half + 1)],
+                    in_=grouped[a][:, 2 * half : 2 * half + 2].rearrange("p g r t -> p (g r t)"),
+                )
 
         ktab = const.tile([P, TILES, 2, PAIRS, 2], F32, name="ktab")
 
-        def finish_table(engine, a0, a1):
+        def finish_table():
             for e in range(2):
-                engine.tensor_tensor(
-                    out=ktab[:, a0:a1, e, :, :],
-                    in0=raw3[:, 1 - e : 3 - e, a0:a1].rearrange("p w a i -> p a i w"),
-                    in1=sgn3[:, 1 - e : 3 - e, a0:a1].rearrange("p w a i -> p a i w"),
+                nc.vector.tensor_tensor(
+                    out=ktab[:, :, e, :, :],
+                    in0=raw3[:, 1 - e : 3 - e].rearrange("p w a i -> p a i w"),
+                    in1=sgn3[:, 1 - e : 3 - e].rearrange("p w a i -> p a i w"),
                     op=ALU.mult,
                 )
 
         res_tiles = {}
+        prod_tiles = {}
         shape = [P, 2, 4, PAIRS, 2]
 
         def matmuls(j, a):
@@ -200,7 +184,7 @@ def tile_attentionblock_pa_kernel(tc, x, w_words, w_scales, q_out, k_out):
                     lhsT=x_codes[a][:, P * g : P * (g + 1)].bitcast(E5M2X4),
                     lhsT_scale=x_scales[a][:, P * g : P * (g + 1)],
                     rhs=w_sb[j][:, g, :].bitcast(E2M1X4),
-                    rhs_scale=planes[j][:, g, :],
+                    rhs_scale=planes[j % PLANES][:, g, :],
                     start=(g == 0),
                     stop=(g == PASSES - 1),
                 )
@@ -214,21 +198,21 @@ def tile_attentionblock_pa_kernel(tc, x, w_words, w_scales, q_out, k_out):
                 op=ALU.mult,
             )
 
-        def out_view(j):
+        def store(j, a0, a1):
             dst = q_out if j < 4 else k_out
             h0 = 4 * (j % 4)
-            return dst[h0 : h0 + 4].rearrange("h (p a) d -> p h a d", a=TILES)
+            nc.scalar.dma_start(
+                out=dst[h0 : h0 + 4].rearrange("h (p a) d -> p h a d", a=TILES)[:, :, a0:a1, :],
+                in_=res_tiles[j][:, :, a0:a1, :],
+            )
 
-        def store(j):
-            nc.scalar.dma_start(out=out_view(j), in_=res_tiles[j][:])
-
-        def single(j, a):
+        def single(j, a, engine):
             acc = matmuls(j, a)
             if j not in res_tiles:
                 res_tiles[j] = outp.tile([P, 4, TILES, P], F32, name="res")
             prod = work1.tile(shape, F32, name="prod1")
             product(acc, a, prod[:])
-            nc.gpsimd.tensor_tensor(
+            engine.tensor_tensor(
                 out=res_tiles[j][:, :, a, :],
                 in0=prod[:, 0].rearrange("p h i w -> p h (i w)"),
                 in1=prod[:, 1].rearrange("p h i w -> p h (i w)"),
@@ -246,7 +230,11 @@ def tile_attentionblock_pa_kernel(tc, x, w_words, w_scales, q_out, k_out):
                 in1=prod[:, 1].rearrange("p h i w -> p h (i w)"),
                 op=ALU.add,
             )
-            nc.scalar.dma_start(out=out_view(j)[:, :, a, :], in_=part[:])
+            dst = q_out if j < 4 else k_out
+            h0 = 4 * (j % 4)
+            nc.scalar.dma_start(
+                out=dst[h0 : h0 + 4].rearrange("h (p a) d -> p h a d", a=TILES)[:, :, a, :], in_=part[:]
+            )
 
         def double(j, a0):
             if j not in res_tiles:
@@ -262,29 +250,29 @@ def tile_attentionblock_pa_kernel(tc, x, w_words, w_scales, q_out, k_out):
                 op=ALU.add,
             )
 
-        finish_table(nc.vector, 0, 1)
-        finish_table(nc.gpsimd, 1, TILES)
-        turn_x(0, 0)
-        quantise(0, 0, 2)
-        turn_x(0, 1)
-        quantise(0, 2, 4)
-        single(0, 0)
+        prepare_x(0)
+        finish_table()
+        single(0, 0, nc.gpsimd)
         prepare_x(1)
-        single(1, 0)
-        single(0, 1)
+        single(1, 0, nc.gpsimd)
+        single(0, 1, nc.gpsimd)
         prepare_x(2)
-        single(1, 1)
-        single(0, 2)
+        single(1, 1, nc.gpsimd)
+        single(0, 2, nc.gpsimd)
         prepare_x(3)
-        single(1, 2)
-        single(0, 3)
-        store(0)
-        single(1, 3)
-        store(1)
+        single(1, 2, nc.gpsimd)
+        single(0, 3, nc.gpsimd)
+        store(0, 0, TILES)
+        load_scales(3)
+        single(1, 3, nc.gpsimd)
+        store(1, 0, TILES)
+        load_scales(4)
         for j in range(2, BLOCKS - 1):
             double(j, 0)
             double(j, 2)
-            store(j)
+            store(j, 0, TILES)
+            if j + PLANES < BLOCKS:
+                load_scales(j + PLANES)
         lone(BLOCKS - 1, 0, nc.gpsimd)
         lone(BLOCKS - 1, 1, nc.gpsimd)
         lone(BLOCKS - 1, 2, nc.vector)

@@ -38,6 +38,12 @@ def tile_attentionblock_pa_kernel(tc, x, w_words, w_scales, q_out, k_out):
         outp = ctx.enter_context(tc.tile_pool(name="outp", bufs=3))
         psum = ctx.enter_context(tc.psum_pool(name="psum", bufs=8))
 
+        dummy = const.tile([P, NB], BF16, name="dummy")
+        nc.gpsimd.memset(dummy[:], 0.0)
+        heat = psum.tile([P, NB], F32, tag="bank", name="heat")
+        for s in range(4):
+            nc.tensor.matmul(out=heat[:], lhsT=dummy[:, 0:P], rhs=dummy[:], start=True, stop=True)
+
         zero = const.tile([P, 1], F32, name="zero")
         nc.vector.memset(zero[:], 0.0)
         warm = const.tile([P, 1], F32, name="warm")
@@ -251,6 +257,11 @@ def tile_attentionblock_pa_kernel(tc, x, w_words, w_scales, q_out, k_out):
             )
 
         prepare_x(0)
+        heat2 = psum.tile([P, NB], F32, tag="bank", name="heat2")
+        for s in range(4):
+            nc.tensor.matmul(
+                out=heat2[:], lhsT=x_sb[0][:, 1024 : 1024 + P], rhs=x_sb[0][:, 1024 : 1024 + NB], start=True, stop=True
+            )
         finish_table()
         single(0, 0, nc.gpsimd)
         prepare_x(1)

@@ -33,8 +33,7 @@ def tile_attentionblock_pa_kernel(tc, x, w_words, w_scales, q_out, k_out):
     nc = tc.nc
     with ExitStack() as ctx:
         const = ctx.enter_context(tc.tile_pool(name="const", bufs=1))
-        work1 = ctx.enter_context(tc.tile_pool(name="work1", bufs=6))
-        work2 = ctx.enter_context(tc.tile_pool(name="work2", bufs=3))
+        work4 = ctx.enter_context(tc.tile_pool(name="work4", bufs=3))
         outp = ctx.enter_context(tc.tile_pool(name="outp", bufs=3))
         psum = ctx.enter_context(tc.psum_pool(name="psum", bufs=8))
 
@@ -85,9 +84,11 @@ def tile_attentionblock_pa_kernel(tc, x, w_words, w_scales, q_out, k_out):
 
         load_x(0, 0, 1024)
         load_x(0, 1024, 2048)
+        load_x(1, 0, 2048)
         load_scales(0)
         load_w(0)
-        load_x(1, 0, 2048)
+        load_x(2, 0, 2048)
+        load_x(3, 0, 2048)
 
         pos_f = const.tile([P, TILES], F32, name="pos_f")
         nc.vector.tensor_copy(out=pos_f[:], in_=pos_i[:])
@@ -135,8 +136,6 @@ def tile_attentionblock_pa_kernel(tc, x, w_words, w_scales, q_out, k_out):
 
         load_scales(1)
         load_w(1)
-        load_x(2, 0, 2048)
-        load_x(3, 0, 2048)
         load_scales(2)
         for j in range(2, BLOCKS):
             load_w(j)
@@ -212,79 +211,62 @@ def tile_attentionblock_pa_kernel(tc, x, w_words, w_scales, q_out, k_out):
                 in_=res_tiles[j][:, :, a0:a1, :],
             )
 
-        def single(j, a, engine):
-            acc = matmuls(j, a)
-            if j not in res_tiles:
-                res_tiles[j] = outp.tile([P, 4, TILES, P], F32, name="res")
-            prod = work1.tile(shape, F32, name="prod1")
-            product(acc, a, prod[:])
-            engine.tensor_tensor(
-                out=res_tiles[j][:, :, a, :],
-                in0=prod[:, 0].rearrange("p h i w -> p h (i w)"),
-                in1=prod[:, 1].rearrange("p h i w -> p h (i w)"),
-                op=ALU.add,
-            )
+        def block(j):
+            res_tiles[j] = outp.tile([P, 4, TILES, P], F32, name="res")
+            prod = work4.tile([P, TILES] + shape[1:], F32, name="prod4")
+            prod_tiles[j] = prod
 
-        def lone(j, a, engine):
+        def bank(j, a):
             acc = matmuls(j, a)
-            prod = work1.tile(shape, F32, name="prod1")
-            product(acc, a, prod[:])
-            part = const.tile([P, 4, P], F32, name="part%d" % a)
-            engine.tensor_tensor(
-                out=part[:],
-                in0=prod[:, 0].rearrange("p h i w -> p h (i w)"),
-                in1=prod[:, 1].rearrange("p h i w -> p h (i w)"),
-                op=ALU.add,
-            )
-            dst = q_out if j < 4 else k_out
-            h0 = 4 * (j % 4)
-            nc.scalar.dma_start(
-                out=dst[h0 : h0 + 4].rearrange("h (p a) d -> p h a d", a=TILES)[:, :, a, :], in_=part[:]
-            )
+            product(acc, a, prod_tiles[j][:, a])
 
-        def double(j, a0):
-            if j not in res_tiles:
-                res_tiles[j] = outp.tile([P, 4, TILES, P], F32, name="res")
-            prod = work2.tile([P, 2] + shape[1:], F32, name="prod2")
-            for t in range(2):
-                acc = matmuls(j, a0 + t)
-                product(acc, a0 + t, prod[:, t])
-            nc.gpsimd.tensor_tensor(
-                out=res_tiles[j][:, :, a0 : a0 + 2, :].rearrange("p h t d -> p t h d"),
-                in0=prod[:, :, 0].rearrange("p t h i w -> p t h (i w)"),
-                in1=prod[:, :, 1].rearrange("p t h i w -> p t h (i w)"),
+        def add(j, a0, a1, engine):
+            prod = prod_tiles[j]
+            engine.tensor_tensor(
+                out=res_tiles[j][:, :, a0:a1, :].rearrange("p h t d -> p t h d"),
+                in0=prod[:, a0:a1, 0].rearrange("p t h i w -> p t h (i w)"),
+                in1=prod[:, a0:a1, 1].rearrange("p t h i w -> p t h (i w)"),
                 op=ALU.add,
             )
 
         prepare_x(0)
+        prepare_x(1)
         heat2 = psum.tile([P, NB], F32, tag="bank", name="heat2")
         for s in range(4):
             nc.tensor.matmul(
                 out=heat2[:], lhsT=x_sb[0][:, 1024 : 1024 + P], rhs=x_sb[0][:, 1024 : 1024 + NB], start=True, stop=True
             )
         finish_table()
-        single(0, 0, nc.gpsimd)
-        prepare_x(1)
-        single(1, 0, nc.gpsimd)
-        single(0, 1, nc.gpsimd)
+        block(0)
+        bank(0, 0)
+        bank(0, 1)
         prepare_x(2)
-        single(1, 1, nc.gpsimd)
-        single(0, 2, nc.gpsimd)
         prepare_x(3)
-        single(1, 2, nc.gpsimd)
-        single(0, 3, nc.gpsimd)
+        bank(0, 2)
+        bank(0, 3)
+        add(0, 0, TILES, nc.gpsimd)
         store(0, 0, TILES)
         load_scales(3)
-        single(1, 3, nc.gpsimd)
-        store(1, 0, TILES)
-        load_scales(4)
-        for j in range(2, BLOCKS - 1):
-            double(j, 0)
-            double(j, 2)
+        for j in range(1, BLOCKS - 1):
+            block(j)
+            for a in range(TILES):
+                bank(j, a)
+            add(j, 0, TILES, nc.gpsimd)
             store(j, 0, TILES)
             if j + PLANES < BLOCKS:
                 load_scales(j + PLANES)
-        lone(BLOCKS - 1, 0, nc.gpsimd)
-        lone(BLOCKS - 1, 1, nc.gpsimd)
-        lone(BLOCKS - 1, 2, nc.vector)
-        lone(BLOCKS - 1, 3, nc.vector)
+        j = BLOCKS - 1
+        block(j)
+        for a in range(TILES):
+            bank(j, a)
+        for a0 in (0, 2):
+            part = const.tile([P, 4, 2, P], F32, name="part%d" % a0)
+            nc.vector.tensor_tensor(
+                out=part[:].rearrange("p h t d -> p t h d"),
+                in0=prod_tiles[j][:, a0 : a0 + 2, 0].rearrange("p t h i w -> p t h (i w)"),
+                in1=prod_tiles[j][:, a0 : a0 + 2, 1].rearrange("p t h i w -> p t h (i w)"),
+                op=ALU.add,
+            )
+            nc.scalar.dma_start(
+                out=k_out[12:16].rearrange("h (p a) d -> p h a d", a=TILES)[:, :, a0 : a0 + 2, :], in_=part[:]
+            )

@@ -85,10 +85,10 @@ def tile_attentionblock_pa_kernel(tc, x, w_words, w_scales, q_out, k_out):
         load_x(0, 0, 1024)
         load_x(0, 1024, 2048)
         load_x(1, 0, 2048)
-        load_scales(0)
-        load_w(0)
         load_x(2, 0, 2048)
         load_x(3, 0, 2048)
+        load_scales(0)
+        load_w(0)
 
         pos_f = const.tile([P, TILES], F32, name="pos_f")
         nc.vector.tensor_copy(out=pos_f[:], in_=pos_i[:])
@@ -229,44 +229,42 @@ def tile_attentionblock_pa_kernel(tc, x, w_words, w_scales, q_out, k_out):
                 op=ALU.add,
             )
 
-        prepare_x(0)
-        prepare_x(1)
-        heat2 = psum.tile([P, NB], F32, tag="bank", name="heat2")
-        for s in range(4):
-            nc.tensor.matmul(
-                out=heat2[:], lhsT=x_sb[0][:, 1024 : 1024 + P], rhs=x_sb[0][:, 1024 : 1024 + NB], start=True, stop=True
+        def lone(j, a0, a1, engine):
+            part = const.tile([P, 4, a1 - a0, P], F32, name="part%d" % a0)
+            engine.tensor_tensor(
+                out=part[:].rearrange("p h t d -> p t h d"),
+                in0=prod_tiles[j][:, a0:a1, 0].rearrange("p t h i w -> p t h (i w)"),
+                in1=prod_tiles[j][:, a0:a1, 1].rearrange("p t h i w -> p t h (i w)"),
+                op=ALU.add,
             )
+            dst = q_out if j < 4 else k_out
+            h0 = 4 * (j % 4)
+            nc.scalar.dma_start(
+                out=dst[h0 : h0 + 4].rearrange("h (p a) d -> p h a d", a=TILES)[:, :, a0:a1, :], in_=part[:]
+            )
+
+        prepare_x(0)
         finish_table()
-        block(0)
-        bank(0, 0)
-        bank(0, 1)
+        prepare_x(1)
         prepare_x(2)
         prepare_x(3)
-        bank(0, 2)
-        bank(0, 3)
-        add(0, 0, TILES, nc.gpsimd)
-        store(0, 0, TILES)
-        load_scales(3)
-        for j in range(1, BLOCKS - 1):
+        for j in range(BLOCKS - 1):
             block(j)
-            for a in range(TILES):
-                bank(j, a)
-            add(j, 0, TILES, nc.gpsimd)
+            bank(j, 0)
+            bank(j, 1)
+            add(j, 0, 2, nc.gpsimd)
+            bank(j, 2)
+            bank(j, 3)
+            add(j, 2, 4, nc.gpsimd)
             store(j, 0, TILES)
             if j + PLANES < BLOCKS:
                 load_scales(j + PLANES)
         j = BLOCKS - 1
         block(j)
-        for a in range(TILES):
-            bank(j, a)
-        for a0 in (0, 2):
-            part = const.tile([P, 4, 2, P], F32, name="part%d" % a0)
-            nc.vector.tensor_tensor(
-                out=part[:].rearrange("p h t d -> p t h d"),
-                in0=prod_tiles[j][:, a0 : a0 + 2, 0].rearrange("p t h i w -> p t h (i w)"),
-                in1=prod_tiles[j][:, a0 : a0 + 2, 1].rearrange("p t h i w -> p t h (i w)"),
-                op=ALU.add,
-            )
-            nc.scalar.dma_start(
-                out=k_out[12:16].rearrange("h (p a) d -> p h a d", a=TILES)[:, :, a0 : a0 + 2, :], in_=part[:]
-            )
+        bank(j, 0)
+        bank(j, 1)
+        lone(j, 0, 2, nc.gpsimd)
+        bank(j, 2)
+        lone(j, 2, 3, nc.gpsimd)
+        bank(j, 3)
+        lone(j, 3, 4, nc.vector)

@@ -82,12 +82,12 @@ def tile_attentionblock_pa_kernel(tc, x, w_words, w_scales, q_out, k_out):
                     in_=w_scales[:, 4 * q : 4 * q + 4, NB * j : NB * (j + 1)].rearrange("g r n -> r g n").bitcast(I32),
                 )
 
+        load_scales(0)
         load_x(0, 0, 1024)
         load_x(0, 1024, 2048)
         load_x(1, 0, 2048)
         load_x(2, 0, 2048)
         load_x(3, 0, 2048)
-        load_scales(0)
         load_w(0)
 
         pos_f = const.tile([P, TILES], F32, name="pos_f")
@@ -230,7 +230,7 @@ def tile_attentionblock_pa_kernel(tc, x, w_words, w_scales, q_out, k_out):
             )
 
         def lone(j, a0, a1, engine):
-            part = const.tile([P, 4, a1 - a0, P], F32, name="part%d" % a0)
+            part = const.tile([P, 4, a1 - a0, P], F32, name="part%d_%d" % (j, a0))
             engine.tensor_tensor(
                 out=part[:].rearrange("p h t d -> p t h d"),
                 in0=prod_tiles[j][:, a0:a1, 0].rearrange("p t h i w -> p t h (i w)"),
@@ -248,23 +248,33 @@ def tile_attentionblock_pa_kernel(tc, x, w_words, w_scales, q_out, k_out):
         prepare_x(1)
         prepare_x(2)
         prepare_x(3)
-        for j in range(BLOCKS - 1):
+        for j in range(BLOCKS - 2):
             block(j)
             bank(j, 0)
             bank(j, 1)
-            add(j, 0, 2, nc.gpsimd)
+            if j == 0:
+                add(j, 0, 2, nc.gpsimd)
             bank(j, 2)
             bank(j, 3)
-            add(j, 2, 4, nc.gpsimd)
+            if j == 0:
+                add(j, 2, 4, nc.gpsimd)
+            else:
+                add(j, 0, 4, nc.gpsimd)
             store(j, 0, TILES)
             if j + PLANES < BLOCKS:
                 load_scales(j + PLANES)
-        j = BLOCKS - 1
+        j = BLOCKS - 2
         block(j)
         bank(j, 0)
         bank(j, 1)
         lone(j, 0, 2, nc.gpsimd)
         bank(j, 2)
-        lone(j, 2, 3, nc.gpsimd)
         bank(j, 3)
+        lone(j, 2, 4, nc.gpsimd)
+        j = BLOCKS - 1
+        block(j)
+        for a in range(TILES):
+            bank(j, a)
+        lone(j, 0, 2, nc.vector)
+        lone(j, 2, 3, nc.vector)
         lone(j, 3, 4, nc.vector)

@@ -50,7 +50,7 @@ def tile_attentionblock_pa_kernel(tc, x, w_words, w_scales, q_out, k_out):
 
         planes = []
         for s in range(PLANES):
-            planes.append(const.tile([P, PASSES, NB], U8, name="plane%d" % s, align_bytes=64))
+            planes.append(const.tile([P, PASSES, NB], U8, name="plane%d" % s, align_bytes=256))
         nc.vector.memset(planes[0][:].bitcast(I32), 0)
 
         pos_i = const.tile([P, TILES], I32, name="pos_i")
@@ -64,7 +64,7 @@ def tile_attentionblock_pa_kernel(tc, x, w_words, w_scales, q_out, k_out):
         for a in range(TILES):
             x_sb.append(const.tile([P, 2048], BF16, name="x_sb%d" % a))
         for j in range(BLOCKS):
-            w_sb.append(const.tile([P, PASSES, 2 * NB], U8, name="w_sb%d" % j, align_bytes=64))
+            w_sb.append(const.tile([P, PASSES, 2 * NB], U8, name="w_sb%d" % j, align_bytes=256))
 
         def load_x(a, c0, c1):
             nc.sync.dma_start(out=x_sb[a][:, c0:c1], in_=x_view[:, a, c0:c1])
@@ -144,9 +144,9 @@ def tile_attentionblock_pa_kernel(tc, x, w_words, w_scales, q_out, k_out):
         x_codes = []
         x_scales = []
         for a in range(TILES):
-            grouped.append(const.tile([P, PASSES, P, 4], BF16, name="grouped%d" % a, align_bytes=64))
-            x_codes.append(const.tile([P, PASSES * P], U32, name="x_codes%d" % a, align_bytes=64))
-            x_scales.append(const.tile([P, PASSES * P], U8, name="x_scales%d" % a, align_bytes=64))
+            grouped.append(const.tile([P, PASSES, P, 4], BF16, name="grouped%d" % a, align_bytes=256))
+            x_codes.append(const.tile([P, PASSES * P], U32, name="x_codes%d" % a, align_bytes=256))
+            x_scales.append(const.tile([P, PASSES * P], U8, name="x_scales%d" % a, align_bytes=256))
 
         def prepare_x(a):
             words = x_sb[a][:].bitcast(F32)

@@ -37,6 +37,13 @@ def tile_attentionblock_pa_kernel(tc, x, w_words, w_scales, q_out, k_out):
         outp = ctx.enter_context(tc.tile_pool(name="outp", bufs=3))
         psum = ctx.enter_context(tc.psum_pool(name="psum", bufs=8))
 
+        ctx.enter_context(tc.manual_schedule(engines={mybir.EngineType.SP}))
+
+        planes = []
+        for s in range(PLANES):
+            planes.append(const.tile([P, PASSES, NB], U8, name="plane%d" % s, align_bytes=256))
+        nc.gpsimd.memset(planes[0][:].bitcast(F32), 0.0)
+
         dummy = const.tile([P, NB], BF16, name="dummy")
         nc.gpsimd.memset(dummy[:], 0.0)
         heat = psum.tile([P, NB], F32, tag="bank", name="heat")
@@ -48,10 +55,6 @@ def tile_attentionblock_pa_kernel(tc, x, w_words, w_scales, q_out, k_out):
         warm = const.tile([P, 1], F32, name="warm")
         nc.scalar.activation(out=warm[:], in_=zero[:], func=ACT.Sin)
 
-        planes = []
-        for s in range(PLANES):
-            planes.append(const.tile([P, PASSES, NB], U8, name="plane%d" % s, align_bytes=256))
-        nc.vector.memset(planes[0][:].bitcast(I32), 0)
 
         pos_i = const.tile([P, TILES], I32, name="pos_i")
         nc.gpsimd.iota(pos_i[:], pattern=[[1, TILES]], base=0, channel_multiplier=TILES)
@@ -82,9 +85,9 @@ def tile_attentionblock_pa_kernel(tc, x, w_words, w_scales, q_out, k_out):
                     in_=w_scales[:, 4 * q : 4 * q + 4, NB * j : NB * (j + 1)].rearrange("g r n -> r g n").bitcast(I32),
                 )
 
-        load_scales(0)
         load_x(0, 0, 1024)
         load_x(0, 1024, 2048)
+        load_scales(0)
         load_x(1, 0, 2048)
         load_x(2, 0, 2048)
         load_x(3, 0, 2048)

@@ -37,7 +37,7 @@ def tile_attentionblock_pa_kernel(tc, x, w_words, w_scales, q_out, k_out):
         outp = ctx.enter_context(tc.tile_pool(name="outp", bufs=3))
         psum = ctx.enter_context(tc.psum_pool(name="psum", bufs=8))
 
-        ctx.enter_context(tc.manual_schedule(engines={mybir.EngineType.SP}))
+        ctx.enter_context(tc.manual_schedule(engines={mybir.EngineType.SP, mybir.EngineType.PE}))
 
         planes = []
         for s in range(PLANES):
@@ -89,9 +89,9 @@ def tile_attentionblock_pa_kernel(tc, x, w_words, w_scales, q_out, k_out):
         load_x(0, 1024, 2048)
         load_scales(0)
         load_x(1, 0, 2048)
+        load_w(0)
         load_x(2, 0, 2048)
         load_x(3, 0, 2048)
-        load_w(0)
 
         pos_f = const.tile([P, TILES], F32, name="pos_f")
         nc.vector.tensor_copy(out=pos_f[:], in_=pos_i[:])
@@ -248,12 +248,18 @@ def tile_attentionblock_pa_kernel(tc, x, w_words, w_scales, q_out, k_out):
 
         prepare_x(0)
         finish_table()
+        heat2 = psum.tile([P, NB], F32, tag="bank", name="heat2")
+        for s in range(2):
+            nc.tensor.matmul(
+                out=heat2[:], lhsT=x_sb[0][:, 1024 : 1024 + P], rhs=x_sb[0][:, 1024 : 1024 + NB], start=True, stop=True
+            )
         prepare_x(1)
-        prepare_x(2)
-        prepare_x(3)
         for j in range(BLOCKS - 2):
             block(j)
             bank(j, 0)
+            if j == 0:
+                prepare_x(2)
+                prepare_x(3)
             bank(j, 1)
             if j == 0:
                 add(j, 0, 2, nc.gpsimd)

@@ -232,18 +232,18 @@ def tile_attentionblock_pa_kernel(tc, x, w_words, w_scales, q_out, k_out):
                 op=ALU.add,
             )
 
-        def lone(j, a0, a1, engine):
-            part = const.tile([P, 4, a1 - a0, P], F32, name="part%d_%d" % (j, a0))
+        def lone(j, a0, a1, engine, c0=0, c1=4):
+            part = const.tile([P, c1 - c0, a1 - a0, P], F32, name="part%d_%d_%d" % (j, a0, c0))
             engine.tensor_tensor(
                 out=part[:].rearrange("p h t d -> p t h d"),
-                in0=prod_tiles[j][:, a0:a1, 0].rearrange("p t h i w -> p t h (i w)"),
-                in1=prod_tiles[j][:, a0:a1, 1].rearrange("p t h i w -> p t h (i w)"),
+                in0=prod_tiles[j][:, a0:a1, 0, c0:c1].rearrange("p t h i w -> p t h (i w)"),
+                in1=prod_tiles[j][:, a0:a1, 1, c0:c1].rearrange("p t h i w -> p t h (i w)"),
                 op=ALU.add,
             )
             dst = q_out if j < 4 else k_out
             h0 = 4 * (j % 4)
             nc.scalar.dma_start(
-                out=dst[h0 : h0 + 4].rearrange("h (p a) d -> p h a d", a=TILES)[:, :, a0:a1, :], in_=part[:]
+                out=dst[h0 + c0 : h0 + c1].rearrange("h (p a) d -> p h a d", a=TILES)[:, :, a0:a1, :], in_=part[:]
             )
 
         prepare_x(0)
@@ -274,16 +274,13 @@ def tile_attentionblock_pa_kernel(tc, x, w_words, w_scales, q_out, k_out):
                 load_scales(j + PLANES)
         j = BLOCKS - 2
         block(j)
-        bank(j, 0)
-        bank(j, 1)
-        lone(j, 0, 2, nc.gpsimd)
-        bank(j, 2)
-        bank(j, 3)
-        lone(j, 2, 4, nc.gpsimd)
+        for a in range(TILES):
+            bank(j, a)
+        lone(j, 0, TILES, nc.gpsimd, 0, 2)
+        lone(j, 0, TILES, nc.gpsimd, 2, 4)
         j = BLOCKS - 1
         block(j)
         for a in range(TILES):
             bank(j, a)
-        lone(j, 0, 2, nc.vector)
-        lone(j, 2, 3, nc.vector)
-        lone(j, 3, 4, nc.vector)
+        for c in range(4):
+            lone(j, 0, TILES, nc.vector, c, c + 1)

@@ -277,7 +277,8 @@ def tile_attentionblock_pa_kernel(tc, x, w_words, w_scales, q_out, k_out):
         for a in range(TILES):
             bank(j, a)
         lone(j, 0, TILES, nc.gpsimd, 0, 2)
-        lone(j, 0, TILES, nc.gpsimd, 2, 4)
+        lone(j, 0, TILES, nc.gpsimd, 2, 3)
+        lone(j, 0, TILES, nc.gpsimd, 3, 4)
         j = BLOCKS - 1
         block(j)
         for a in range(TILES):

@@ -91,7 +91,8 @@ def tile_attentionblock_pa_kernel(tc, x, w_words, w_scales, q_out, k_out):
         load_x(1, 0, 2048)
         load_w(0)
         load_x(2, 0, 2048)
-        load_x(3, 0, 2048)
+        load_x(3, 0, 1024)
+        load_x(3, 1024, 2048)
 
         pos_f = const.tile([P, TILES], F32, name="pos_f")
         nc.vector.tensor_copy(out=pos_f[:], in_=pos_i[:])

@@ -101,40 +101,28 @@ def tile_attentionblock_pa_kernel(tc, x, w_words, w_scales, q_out, k_out):
             nc.vector.tensor_scalar(
                 out=ang_hi[:, :, hi], in0=pos_f[:], scalar1=theta(8 * hi), scalar2=None, op0=ALU.mult
             )
-        ang = const.tile([P, 2, TILES, 8, 8], F32, name="ang")
+        ang3 = const.tile([P, 3, TILES, 8, 8], F32, name="ang3")
         for lo in range(8):
             nc.vector.tensor_scalar(
-                out=ang[:, 1, :, :, lo], in0=ang_hi[:], scalar1=theta(lo), scalar2=None, op0=ALU.mult
+                out=ang3[:, 2, :, :, lo], in0=ang_hi[:], scalar1=theta(lo), scalar2=None, op0=ALU.mult
             )
+        nc.vector.tensor_scalar(out=ang3[:, 1], in0=ang3[:, 2], scalar1=math.pi / 2.0, scalar2=None, op0=ALU.add)
+        nc.vector.tensor_scalar(out=ang3[:, 0], in0=ang3[:, 2], scalar1=math.pi, scalar2=None, op0=ALU.add)
+        ang_flat = ang3[:].rearrange("p f a h l -> p (f a h l)")
+        turns = const.tile([P, 3 * TILES * PAIRS], I32, name="turns")
         nc.vector.tensor_scalar(
-            out=ang[:, 0], in0=ang[:, 1], scalar1=math.pi / 2.0, scalar2=None, op0=ALU.add
+            out=turns[:], in0=ang_flat, scalar1=1.0 / (2.0 * math.pi), scalar2=None, op0=ALU.mult
         )
-        ang_flat = ang[:].rearrange("p f a h l -> p (f a h l)")
-        half_w = TILES * PAIRS
-        turns = const.tile([P, 2 * half_w], I32, name="turns")
-        nc.vector.tensor_scalar(
-            out=turns[:], in0=ang_flat, scalar1=1.0 / math.pi, scalar2=0.25, op0=ALU.mult, op1=ALU.add
-        )
-        red = const.tile([P, 2 * half_w], F32, name="red")
+        red = const.tile([P, 3, TILES, PAIRS], F32, name="red")
         nc.vector.scalar_tensor_tensor(
-            out=red[:], in0=turns[:], scalar=-math.pi, in1=ang_flat, op0=ALU.mult, op1=ALU.add
-        )
-        raw3 = const.tile([P, 3, TILES, PAIRS], F32, name="raw3")
-        sgn3 = const.tile([P, 3, TILES, PAIRS], F32, name="sgn3")
-        nc.scalar.activation(out=raw3[:, 1:3].rearrange("p f a i -> p (f a i)"), in_=red[:], func=ACT.Sin)
-        nc.scalar.activation(
-            out=raw3[:, 0].rearrange("p a i -> p (a i)"), in_=red[:, half_w : 2 * half_w], func=ACT.Sin
-        )
-        par = const.tile([P, 2 * half_w], I32, name="par")
-        nc.vector.tensor_scalar(out=par[:], in0=turns[:], scalar1=1, scalar2=None, op0=ALU.bitwise_and)
-        nc.vector.tensor_scalar(
-            out=sgn3[:, 1:3].rearrange("p f a i -> p (f a i)"), in0=par[:], scalar1=-2.0, scalar2=1.0,
+            out=red[:].rearrange("p f a i -> p (f a i)"), in0=turns[:], scalar=-2.0 * math.pi, in1=ang_flat,
             op0=ALU.mult, op1=ALU.add,
         )
-        nc.vector.tensor_scalar(
-            out=sgn3[:, 0].rearrange("p a i -> p (a i)"), in0=par[:, half_w : 2 * half_w], scalar1=2.0,
-            scalar2=-1.0, op0=ALU.mult, op1=ALU.add,
-        )
+        ktab = const.tile([P, TILES, 2, PAIRS, 2], F32, name="ktab")
+        for e in range(2):
+            nc.scalar.activation(
+                out=ktab[:, :, e, :, :], in_=red[:, 1 - e : 3 - e].rearrange("p w a i -> p a i w"), func=ACT.Sin
+            )
         nc.vector.memset(planes[1][:].bitcast(I32), 0)
         nc.vector.memset(planes[2][:].bitcast(I32), 0)
 
@@ -168,17 +156,6 @@ def tile_attentionblock_pa_kernel(tc, x, w_words, w_scales, q_out, k_out):
                     out=x_codes[a][:, 256 * half : 256 * (half + 1)].bitcast(E5M2X4),
                     scales=x_scales[a][:, 256 * half : 256 * (half + 1)],
                     in_=grouped[a][:, 2 * half : 2 * half + 2].rearrange("p g r t -> p (g r t)"),
-                )
-
-        ktab = const.tile([P, TILES, 2, PAIRS, 2], F32, name="ktab")
-
-        def finish_table():
-            for e in range(2):
-                nc.vector.tensor_tensor(
-                    out=ktab[:, :, e, :, :],
-                    in0=raw3[:, 1 - e : 3 - e].rearrange("p w a i -> p a i w"),
-                    in1=sgn3[:, 1 - e : 3 - e].rearrange("p w a i -> p a i w"),
-                    op=ALU.mult,
                 )
 
         res_tiles = {}
@@ -248,7 +225,6 @@ def tile_attentionblock_pa_kernel(tc, x, w_words, w_scales, q_out, k_out):
             )
 
         prepare_x(0)
-        finish_table()
         heat2 = psum.tile([P, NB], F32, tag="bank", name="heat2")
         for s in range(2):
             nc.tensor.matmul(

@@ -43,9 +43,13 @@ def tile_attentionblock_pa_kernel(tc, x, w_words, w_scales, q_out, k_out):
         for s in range(PLANES):
             planes.append(const.tile([P, PASSES, NB], U8, name="plane%d" % s, align_bytes=256))
         nc.gpsimd.memset(planes[0][:].bitcast(F32), 0.0)
+        pos_f = const.tile([P, TILES], F32, name="pos_f")
+        nc.gpsimd.iota(
+            pos_f[:], pattern=[[1, TILES]], base=0, channel_multiplier=TILES, allow_small_or_imprecise_dtypes=True
+        )
 
         dummy = const.tile([P, NB], BF16, name="dummy")
-        nc.gpsimd.memset(dummy[:], 0.0)
+        nc.vector.memset(dummy[:], 0.0)
         heat = psum.tile([P, NB], F32, tag="bank", name="heat")
         for s in range(4):
             nc.tensor.matmul(out=heat[:], lhsT=dummy[:, 0:P], rhs=dummy[:], start=True, stop=True)
@@ -56,8 +60,6 @@ def tile_attentionblock_pa_kernel(tc, x, w_words, w_scales, q_out, k_out):
         nc.scalar.activation(out=warm[:], in_=zero[:], func=ACT.Sin)
 
 
-        pos_i = const.tile([P, TILES], I32, name="pos_i")
-        nc.gpsimd.iota(pos_i[:], pattern=[[1, TILES]], base=0, channel_multiplier=TILES)
         ident = const.tile([P, P], F32, name="ident")
         make_identity(nc, ident[:])
 
@@ -94,8 +96,6 @@ def tile_attentionblock_pa_kernel(tc, x, w_words, w_scales, q_out, k_out):
         load_x(3, 0, 1024)
         load_x(3, 1024, 2048)
 
-        pos_f = const.tile([P, TILES], F32, name="pos_f")
-        nc.vector.tensor_copy(out=pos_f[:], in_=pos_i[:])
         ang_hi = const.tile([P, TILES, 8], F32, name="ang_hi")
         for hi in range(8):
             nc.vector.tensor_scalar(

@@ -43,9 +43,10 @@ def tile_attentionblock_pa_kernel(tc, x, w_words, w_scales, q_out, k_out):
         for s in range(PLANES):
             planes.append(const.tile([P, PASSES, NB], U8, name="plane%d" % s, align_bytes=256))
         nc.gpsimd.memset(planes[0][:].bitcast(F32), 0.0)
-        pos_f = const.tile([P, TILES], F32, name="pos_f")
+        angp = const.tile([P, 8, 8, TILES], F32, name="angp")
         nc.gpsimd.iota(
-            pos_f[:], pattern=[[1, TILES]], base=0, channel_multiplier=TILES, allow_small_or_imprecise_dtypes=True
+            angp[:, 0, 0, :], pattern=[[1, TILES]], base=0, channel_multiplier=TILES,
+            allow_small_or_imprecise_dtypes=True,
         )
 
         dummy = const.tile([P, NB], BF16, name="dummy")
@@ -54,10 +55,8 @@ def tile_attentionblock_pa_kernel(tc, x, w_words, w_scales, q_out, k_out):
         for s in range(4):
             nc.tensor.matmul(out=heat[:], lhsT=dummy[:, 0:P], rhs=dummy[:], start=True, stop=True)
 
-        zero = const.tile([P, 1], F32, name="zero")
-        nc.vector.memset(zero[:], 0.0)
         warm = const.tile([P, 1], F32, name="warm")
-        nc.scalar.activation(out=warm[:], in_=zero[:], func=ACT.Sin)
+        nc.scalar.activation(out=warm[:], in_=dummy[:, 0:1], func=ACT.Sin)
 
 
         ident = const.tile([P, P], F32, name="ident")
@@ -96,19 +95,19 @@ def tile_attentionblock_pa_kernel(tc, x, w_words, w_scales, q_out, k_out):
         load_x(3, 0, 1024)
         load_x(3, 1024, 2048)
 
-        ang_hi = const.tile([P, TILES, 8], F32, name="ang_hi")
-        for hi in range(8):
+        for lo in range(1, 8):
             nc.vector.tensor_scalar(
-                out=ang_hi[:, :, hi], in0=pos_f[:], scalar1=theta(8 * hi), scalar2=None, op0=ALU.mult
+                out=angp[:, 0, lo, :], in0=angp[:, 0, 0, :], scalar1=theta(lo), scalar2=None, op0=ALU.mult
             )
-        ang3 = const.tile([P, 3, TILES, 8, 8], F32, name="ang3")
-        for lo in range(8):
+        for hi in range(1, 8):
+            nc.vector.tensor_scalar(out=angp[:, hi], in0=angp[:, 0], scalar1=theta(8 * hi), scalar2=None, op0=ALU.mult)
+        ang3 = const.tile([P, 3, TILES, PAIRS], F32, name="ang3")
+        by_tile = angp[:].rearrange("p h l a -> p a (h l)")
+        for f in range(3):
             nc.vector.tensor_scalar(
-                out=ang3[:, 2, :, :, lo], in0=ang_hi[:], scalar1=theta(lo), scalar2=None, op0=ALU.mult
+                out=ang3[:, f], in0=by_tile, scalar1=(2 - f) * math.pi / 2.0, scalar2=None, op0=ALU.add
             )
-        nc.vector.tensor_scalar(out=ang3[:, 1], in0=ang3[:, 2], scalar1=math.pi / 2.0, scalar2=None, op0=ALU.add)
-        nc.vector.tensor_scalar(out=ang3[:, 0], in0=ang3[:, 2], scalar1=math.pi, scalar2=None, op0=ALU.add)
-        ang_flat = ang3[:].rearrange("p f a h l -> p (f a h l)")
+        ang_flat = ang3[:].rearrange("p f a i -> p (f a i)")
         turns = const.tile([P, 3 * TILES * PAIRS], I32, name="turns")
         nc.vector.tensor_scalar(
             out=turns[:], in0=ang_flat, scalar1=1.0 / (2.0 * math.pi), scalar2=None, op0=ALU.mult
@@ -118,10 +117,10 @@ def tile_attentionblock_pa_kernel(tc, x, w_words, w_scales, q_out, k_out):
             out=red[:].rearrange("p f a i -> p (f a i)"), in0=turns[:], scalar=-2.0 * math.pi, in1=ang_flat,
             op0=ALU.mult, op1=ALU.add,
         )
-        ktab = const.tile([P, TILES, 2, PAIRS, 2], F32, name="ktab")
+        ktab = const.tile([P, 2, TILES, PAIRS, 2], F32, name="ktab")
         for e in range(2):
             nc.scalar.activation(
-                out=ktab[:, :, e, :, :], in_=red[:, 1 - e : 3 - e].rearrange("p w a i -> p a i w"), func=ACT.Sin
+                out=ktab[:, e], in_=red[:, 1 - e : 3 - e].rearrange("p w a i -> p a i w"), func=ACT.Sin
             )
         nc.vector.memset(planes[1][:].bitcast(I32), 0)
         nc.vector.memset(planes[2][:].bitcast(I32), 0)
@@ -180,7 +179,7 @@ def tile_attentionblock_pa_kernel(tc, x, w_words, w_scales, q_out, k_out):
             nc.vector.tensor_tensor(
                 out=out_ap,
                 in0=acc[:].rearrange("p (h i e) -> p e h i", h=4, i=PAIRS, e=2).unsqueeze(4).to_broadcast(shape),
-                in1=ktab[:, a].unsqueeze(2).to_broadcast(shape),
+                in1=ktab[:, :, a].unsqueeze(2).to_broadcast(shape),
                 op=ALU.mult,
             )
 

@@ -254,10 +254,13 @@ def tile_attentionblock_pa_kernel(tc, x, w_words, w_scales, q_out, k_out):
             bank(j, a)
         lone(j, 0, TILES, nc.gpsimd, 0, 2)
         lone(j, 0, TILES, nc.gpsimd, 2, 3)
-        lone(j, 0, TILES, nc.gpsimd, 3, 4)
+        ctx.enter_context(
+            tc.manual_schedule(engines={mybir.EngineType.SP, mybir.EngineType.PE, mybir.EngineType.DVE})
+        )
         j = BLOCKS - 1
         block(j)
         for a in range(TILES):
             bank(j, a)
+        lone(j - 1, 0, TILES, nc.vector, 3, 4)
         for c in range(4):
             lone(j, 0, TILES, nc.vector, c, c + 1)

import math
from contextlib import ExitStack

import concourse.mybir as mybir
from concourse.masks import make_identity

FLOPS = 2 * 512 * 2048 * 4096

F32 = mybir.dt.float32
BF16 = mybir.dt.bfloat16
I32 = mybir.dt.int32
U32 = mybir.dt.uint32
U8 = mybir.dt.uint8
E5M2X4 = mybir.dt.float8_e5m2_x4
E2M1X4 = mybir.dt.float4_e2m1fn_x4
ALU = mybir.AluOpType
ACT = mybir.ActivationFunctionType

P = 128
TILES = 4
PASSES = 4
BLOCKS = 8
NB = 512
PAIRS = 64
PLANES = 3


def theta(e):
    return 10000.0 ** (-e / 64.0)


def tile_attentionblock_pa_kernel(tc, x, w_words, w_scales, q_out, k_out):
    nc = tc.nc
    with ExitStack() as ctx:
        const = ctx.enter_context(tc.tile_pool(name="const", bufs=1))
        work4 = ctx.enter_context(tc.tile_pool(name="work4", bufs=3))
        outp = ctx.enter_context(tc.tile_pool(name="outp", bufs=3))
        psum = ctx.enter_context(tc.psum_pool(name="psum", bufs=8))

        ctx.enter_context(tc.manual_schedule(engines={mybir.EngineType.SP, mybir.EngineType.PE}))

        planes = []
        for s in range(PLANES):
            planes.append(const.tile([P, PASSES, NB], U8, name="plane%d" % s, align_bytes=256))
        nc.gpsimd.memset(planes[0][:].bitcast(F32), 0.0)
        angp = const.tile([P, 8, 8, TILES], F32, name="angp")
        nc.gpsimd.iota(
            angp[:, 0, 0, :], pattern=[[1, TILES]], base=0, channel_multiplier=TILES,
            allow_small_or_imprecise_dtypes=True,
        )

        dummy = const.tile([P, NB], BF16, name="dummy")
        nc.vector.memset(dummy[:], 0.0)
        heat = psum.tile([P, NB], F32, tag="bank", name="heat")
        for s in range(4):
            nc.tensor.matmul(out=heat[:], lhsT=dummy[:, 0:P], rhs=dummy[:], start=True, stop=True)

        warm = const.tile([P, 1], F32, name="warm")
        nc.scalar.activation(out=warm[:], in_=dummy[:, 0:1], func=ACT.Sin)


        ident = const.tile([P, P], F32, name="ident")
        make_identity(nc, ident[:])

        x_view = x.rearrange("(p a) k -> p a k", a=TILES)
        x_sb = []
        w_sb = []
        for a in range(TILES):
            x_sb.append(const.tile([P, 2048], BF16, name="x_sb%d" % a))
        for j in range(BLOCKS):
            w_sb.append(const.tile([P, PASSES, 2 * NB], U8, name="w_sb%d" % j, align_bytes=256))

        def load_x(a, c0, c1):
            nc.sync.dma_start(out=x_sb[a][:, c0:c1], in_=x_view[:, a, c0:c1])

        def load_w(j):
            nc.sync.dma_start(
                out=w_sb[j][:].bitcast(I32),
                in_=w_words[:, :, 2 * NB * j : 2 * NB * (j + 1)].rearrange("g p n -> p g n").bitcast(I32),
            )

        def load_scales(j):
            for q in range(4):
                nc.sync.dma_start(
                    out=planes[j % PLANES][32 * q : 32 * q + 4, :, :].bitcast(I32),
                    in_=w_scales[:, 4 * q : 4 * q + 4, NB * j : NB * (j + 1)].rearrange("g r n -> r g n").bitcast(I32),
                )

        load_x(0, 0, 1024)
        load_x(0, 1024, 2048)
        load_scales(0)
        load_x(1, 0, 2048)
        load_w(0)
        load_x(2, 0, 2048)
        load_x(3, 0, 1024)
        load_x(3, 1024, 2048)

        for lo in range(1, 8):
            nc.vector.tensor_scalar(
                out=angp[:, 0, lo, :], in0=angp[:, 0, 0, :], scalar1=theta(lo), scalar2=None, op0=ALU.mult
            )
        for hi in range(1, 8):
            nc.vector.tensor_scalar(out=angp[:, hi], in0=angp[:, 0], scalar1=theta(8 * hi), scalar2=None, op0=ALU.mult)
        ang3 = const.tile([P, 3, TILES, PAIRS], F32, name="ang3")
        by_tile = angp[:].rearrange("p h l a -> p a (h l)")
        for f in range(3):
            nc.vector.tensor_scalar(
                out=ang3[:, f], in0=by_tile, scalar1=(2 - f) * math.pi / 2.0, scalar2=None, op0=ALU.add
            )
        ang_flat = ang3[:].rearrange("p f a i -> p (f a i)")
        turns = const.tile([P, 3 * TILES * PAIRS], I32, name="turns")
        nc.vector.tensor_scalar(
            out=turns[:], in0=ang_flat, scalar1=1.0 / (2.0 * math.pi), scalar2=None, op0=ALU.mult
        )
        red = const.tile([P, 3, TILES, PAIRS], F32, name="red")
        nc.vector.scalar_tensor_tensor(
            out=red[:].rearrange("p f a i -> p (f a i)"), in0=turns[:], scalar=-2.0 * math.pi, in1=ang_flat,
            op0=ALU.mult, op1=ALU.add,
        )
        ktab = const.tile([P, 2, TILES, PAIRS, 2], F32, name="ktab")
        for e in range(2):
            nc.scalar.activation(
                out=ktab[:, e], in_=red[:, 1 - e : 3 - e].rearrange("p w a i -> p a i w"), func=ACT.Sin
            )
        nc.vector.memset(planes[1][:].bitcast(I32), 0)
        nc.vector.memset(planes[2][:].bitcast(I32), 0)

        load_scales(1)
        load_w(1)
        load_scales(2)
        for j in range(2, BLOCKS):
            load_w(j)

        grouped = []
        x_codes = []
        x_scales = []
        for a in range(TILES):
            grouped.append(const.tile([P, PASSES, P, 4], BF16, name="grouped%d" % a, align_bytes=256))
            x_codes.append(const.tile([P, PASSES * P], U32, name="x_codes%d" % a, align_bytes=256))
            x_scales.append(const.tile([P, PASSES * P], U8, name="x_scales%d" % a, align_bytes=256))

        def prepare_x(a):
            words = x_sb[a][:].bitcast(F32)
            for half in range(2):
                xt = psum.tile([P, 2, 2, P], F32, tag="bank", name="xt")
                for g2 in range(2):
                    g = 2 * half + g2
                    for u in range(2):
                        nc.tensor.transpose(xt[:, g2, u, :], words[:, 256 * g + u : 256 * (g + 1) : 2], ident[:])
                nc.scalar.copy(
                    out=grouped[a][:, 2 * half : 2 * half + 2].bitcast(F32),
                    in_=xt[:].rearrange("p g u r -> p g r u"),
                )
                nc.vector.quantize_mx(
                    out=x_codes[a][:, 256 * half : 256 * (half + 1)].bitcast(E5M2X4),
                    scales=x_scales[a][:, 256 * half : 256 * (half + 1)],
                    in_=grouped[a][:, 2 * half : 2 * half + 2].rearrange("p g r t -> p (g r t)"),
                )

        res_tiles = {}
        prod_tiles = {}
        shape = [P, 2, 4, PAIRS, 2]

        def matmuls(j, a):
            acc = psum.tile([P, NB], F32, tag="bank", name="acc")
            for g in range(PASSES):
                nc.tensor.matmul_mx(
                    out=acc[:],
                    lhsT=x_codes[a][:, P * g : P * (g + 1)].bitcast(E5M2X4),
                    lhsT_scale=x_scales[a][:, P * g : P * (g + 1)],
                    rhs=w_sb[j][:, g, :].bitcast(E2M1X4),
                    rhs_scale=planes[j % PLANES][:, g, :],
                    start=(g == 0),
                    stop=(g == PASSES - 1),
                )
            return acc

        def product(acc, a, out_ap):
            nc.vector.tensor_tensor(
                out=out_ap,
                in0=acc[:].rearrange("p (h i e) -> p e h i", h=4, i=PAIRS, e=2).unsqueeze(4).to_broadcast(shape),
                in1=ktab[:, :, a].unsqueeze(2).to_broadcast(shape),
                op=ALU.mult,
            )

        def store(j, a0, a1):
            dst = q_out if j < 4 else k_out
            h0 = 4 * (j % 4)
            nc.scalar.dma_start(
                out=dst[h0 : h0 + 4].rearrange("h (p a) d -> p h a d", a=TILES)[:, :, a0:a1, :],
                in_=res_tiles[j][:, :, a0:a1, :],
            )

        def block(j):
            res_tiles[j] = outp.tile([P, 4, TILES, P], F32, name="res")
            prod = work4.tile([P, TILES] + shape[1:], F32, name="prod4")
            prod_tiles[j] = prod

        def bank(j, a):
            acc = matmuls(j, a)
            product(acc, a, prod_tiles[j][:, a])

        def add(j, a0, a1, engine):
            prod = prod_tiles[j]
            engine.tensor_tensor(
                out=res_tiles[j][:, :, a0:a1, :].rearrange("p h t d -> p t h d"),
                in0=prod[:, a0:a1, 0].rearrange("p t h i w -> p t h (i w)"),
                in1=prod[:, a0:a1, 1].rearrange("p t h i w -> p t h (i w)"),
                op=ALU.add,
            )

        def lone(j, a0, a1, engine, c0=0, c1=4):
            part = const.tile([P, c1 - c0, a1 - a0, P], F32, name="part%d_%d_%d" % (j, a0, c0))
            engine.tensor_tensor(
                out=part[:].rearrange("p h t d -> p t h d"),
                in0=prod_tiles[j][:, a0:a1, 0, c0:c1].rearrange("p t h i w -> p t h (i w)"),
                in1=prod_tiles[j][:, a0:a1, 1, c0:c1].rearrange("p t h i w -> p t h (i w)"),
                op=ALU.add,
            )
            dst = q_out if j < 4 else k_out
            h0 = 4 * (j % 4)
            nc.scalar.dma_start(
                out=dst[h0 + c0 : h0 + c1].rearrange("h (p a) d -> p h a d", a=TILES)[:, :, a0:a1, :], in_=part[:]
            )

        prepare_x(0)
        heat2 = psum.tile([P, NB], F32, tag="bank", name="heat2")
        for s in range(2):
            nc.tensor.matmul(
                out=heat2[:], lhsT=x_sb[0][:, 1024 : 1024 + P], rhs=x_sb[0][:, 1024 : 1024 + NB], start=True, stop=True
            )
        prepare_x(1)
        for j in range(BLOCKS - 2):
            block(j)
            bank(j, 0)
            if j == 0:
                prepare_x(2)
                prepare_x(3)
            bank(j, 1)
            if j == 0:
                add(j, 0, 2, nc.gpsimd)
            bank(j, 2)
            bank(j, 3)
            if j == 0:
                add(j, 2, 4, nc.gpsimd)
            else:
                add(j, 0, 4, nc.gpsimd)
            store(j, 0, TILES)
            if j + PLANES < BLOCKS:
                load_scales(j + PLANES)
        j = BLOCKS - 2
        block(j)
        for a in range(TILES):
            bank(j, a)
        lone(j, 0, TILES, nc.gpsimd, 0, 2)
        lone(j, 0, TILES, nc.gpsimd, 2, 3)
        ctx.enter_context(
            tc.manual_schedule(engines={mybir.EngineType.SP, mybir.EngineType.PE, mybir.EngineType.DVE})
        )
        j = BLOCKS - 1
        block(j)
        for a in range(TILES):
            bank(j, a)
        lone(j - 1, 0, TILES, nc.vector, 3, 4)
        for c in range(4):
            lone(j, 0, TILES, nc.vector, c, c + 1)
